import numpy as np
import ml_dtypes


def mxq(x, axis, fmt="e4m3"):
    dtype, down = {"e4m3": (ml_dtypes.float8_e4m3fn, 7), "e5m2": (ml_dtypes.float8_e5m2, 14)}[fmt]
    v = np.moveaxis(np.asarray(x, np.float32).astype(ml_dtypes.bfloat16).astype(np.float64), axis, -1)
    blocks = v.reshape(v.shape[:-1] + (-1, 32))
    amax = np.abs(blocks).max(-1, keepdims=True)
    byte = np.maximum(np.where(amax > 0, np.frexp(amax)[1] - 1 + 127, 0) - down, 1)
    scale = np.exp2(byte - 127.0)
    codes = (blocks / scale).astype(np.float32).astype(dtype).astype(np.float64)
    return np.moveaxis((codes * scale).reshape(v.shape), -1, axis)


WIDE = False


def mx_kscale(k):
    if not WIDE:
        return np.ones(k)
    levels = np.array([10, -10, 5, -5, 0])
    a = np.random.permutation(np.resize(levels, k // 512 * 4)).reshape(k // 512, 4)
    idx = np.arange(k)
    return np.exp2(a[idx // 512, idx % 128 // 32])


BF16 = ml_dtypes.bfloat16


def bf(x):
    return np.asarray(x, np.float32).astype(BF16)


def f64(x):
    return np.asarray(x).astype(np.float64)


E2M1 = np.array([0.0, 0.5, 1.0, 1.5, 2.0, 3.0, 4.0, 6.0, -0.0, -0.5, -1.0, -1.5, -2.0, -3.0, -4.0, -6.0])


def pack_weight(w, fmt):
    k, n = w.shape
    w = f64(bf(w)).reshape(k // 32, 32, n)
    amax = np.abs(w).max(1)
    if fmt == "e4m3":
        byte = np.frexp(amax)[1] - 1 + 127 - 7
    else:
        mant, ex = np.frexp(amax / 6.0)
        byte = np.where(mant > 0.5, ex, ex - 1) + 127
    byte = np.clip(np.where(amax > 0, byte, 1), 1, 254)
    scaled = (w * np.exp2(127.0 - byte)[:, None, :]).reshape(k, n).astype(np.float32)
    by_word = np.ascontiguousarray(scaled.reshape(k // 512, 128, 4, n).transpose(0, 1, 3, 2))
    if fmt == "e4m3":
        words = by_word.astype(ml_dtypes.float8_e4m3fn).view(np.uint8)
    else:
        c = by_word.astype(ml_dtypes.float4_e2m1fn).view(np.uint8) & 0xF
        words = c[..., 0::2] | (c[..., 1::2] << 4)
    return np.ascontiguousarray(words), np.ascontiguousarray(byte.astype(np.uint8).reshape(k // 512, 16, n))


def unpack_weight(words, scales, fmt):
    g, p, n, _ = words.shape
    if fmt == "e4m3":
        vals = np.ascontiguousarray(words).view(ml_dtypes.float8_e4m3fn).astype(np.float64)
    else:
        nib = np.empty((g, p, n, 4), np.uint8)
        nib[..., 0::2] = words & 0xF
        nib[..., 1::2] = words >> 4
        vals = E2M1[nib]
    vals = vals * np.repeat(np.exp2(scales.astype(np.float64) - 127.0), 8, axis=1)[..., None]
    return vals.transpose(0, 1, 3, 2).reshape(g * 512, n)


B, T, D, H = 2, 1024, 512, 2048
R = B * T
EPS = 1e-5
FMT = "e4m3"


def sigmoid(v):
    return 1.0 / (1.0 + np.exp(-v))


def layer_norm(x, g, b):
    mu = x.mean(-1, keepdims=True)
    var = np.square(x - mu).mean(-1, keepdims=True)
    return (x - mu) / np.sqrt(var + EPS) * g + b


def setup_inputs():
    s, t = mx_kscale(D), mx_kscale(D)
    n = np.random.standard_normal
    x = bf(n((B, T, D)))
    yt = bf(n((B, T, D)) * 0.5 * t)
    ln1_g = bf((1.0 + 0.2 * n(D)) * s)
    ln1_b = bf(0.3 * n(D) * s)
    Wq_words, Wq_scales = pack_weight(n((D, D)) * 1.5 / np.sqrt(D) / s[:, None], FMT)
    bq = bf(0.3 * n(D))
    Wo_words, Wo_scales = pack_weight(n((D, D)) * 2.5 / np.sqrt(D) / t[:, None], FMT)
    bo = bf(0.3 * n(D))
    return {"x": x, "yt": yt,
            "ln1_g": ln1_g, "ln1_b": ln1_b,
            "Wq_words": Wq_words, "Wq_scales": Wq_scales, "bq": bq,
            "Wo_words": Wo_words, "Wo_scales": Wo_scales, "bo": bo}


def reference(x, yt, ln1_g, ln1_b, Wq_words, Wq_scales, bq, Wo_words, Wo_scales, bo):
    xr = f64(x).reshape(R, D)
    h = layer_norm(xr, f64(ln1_g), f64(ln1_b))
    q = (mxq(h, 1, "e4m3") @ unpack_weight(Wq_words, Wq_scales, FMT)) + f64(bq)
    y = sigmoid(q) * f64(yt).reshape(R, D)
    attn = (mxq(y, 1, "e4m3") @ unpack_weight(Wo_words, Wo_scales, FMT)) + f64(bo)
    return (attn + xr).reshape(B, T, D)

@@ -1,0 +1,219 @@
+from contextlib import ExitStack
+
+import concourse.mybir as mybir
+from concourse.masks import make_identity
+
+F32 = mybir.dt.float32
+BF16 = mybir.dt.bfloat16
+I32 = mybir.dt.int32
+U32 = mybir.dt.uint32
+U8 = mybir.dt.uint8
+FP8X4 = mybir.dt.float8_e4m3fn_x4
+ACT = mybir.ActivationFunctionType
+ALU = mybir.AluOpType
+
+P = 128
+D = 512
+PACK = 4
+ROWS = 2048
+TILES = ROWS // P
+CHUNK = 4
+CHUNKS = TILES // CHUNK
+CHUNK_ROWS = CHUNK * P
+HALF_ROWS = CHUNK_ROWS // 2
+EPS = 1e-5
+
+FLOPS = 2 * 2 * ROWS * D * D
+
+
+def load_weight(nc, words_dram, scales_dram, words, plane):
+    scale_rows = scales_dram.rearrange("g q n -> (g q) n")
+    for quadrant in range(4):
+        nc.sync.dma_start(
+            out=plane[32 * quadrant : 32 * quadrant + 4, :].bitcast(I32),
+            in_=scale_rows[4 * quadrant : 4 * quadrant + 4, :].bitcast(I32),
+        )
+    nc.sync.dma_start(
+        out=words[:].bitcast(I32),
+        in_=words_dram.rearrange("g p n t -> (g p) (n t)").bitcast(I32),
+    )
+
+
+def tile_attentionfreetransformerencoder_pb_kernel(
+    tc, x, yt, ln1_g, ln1_b, Wq_words, Wq_scales, bq, Wo_words, Wo_scales, bo, out
+):
+    nc = tc.nc
+    x_rows = x.flatten_outer_dims().rearrange("(p i) k -> p i k", i=TILES)
+    yt_rows = yt.flatten_outer_dims().rearrange("(p i) k -> p i k", i=TILES)
+    out_rows = out.flatten_outer_dims().rearrange("(p i) n -> p i n", i=TILES)
+
+    with ExitStack() as ctx:
+        keep = ctx.enter_context(tc.tile_pool(name="keep", bufs=1))
+        norm = ctx.enter_context(tc.tile_pool(name="norm", bufs=CHUNKS))
+        gate = ctx.enter_context(tc.tile_pool(name="gate", bufs=2))
+        psum = ctx.enter_context(tc.psum_pool(name="psum", bufs=2))
+
+        wq_plane = keep.tile([P, D], U8, align_bytes=64)
+        wo_plane = keep.tile([P, D], U8, align_bytes=64)
+        nc.vector.memset(wq_plane[:].bitcast(I32), 0)
+        nc.vector.memset(wo_plane[:].bitcast(I32), 0)
+        wq_words = keep.tile([P, D * PACK], U8, align_bytes=64)
+        wo_words = keep.tile([P, D * PACK], U8, align_bytes=64)
+
+        x_sb = []
+        yt_sb = []
+        for c in range(CHUNKS):
+            x_chunk = keep.tile([P, CHUNK, D], BF16, name="x%d" % c)
+            x_sb.append(x_chunk)
+            yt_chunk = keep.tile([P, CHUNK, D], BF16, name="yt%d" % c)
+            yt_sb.append(yt_chunk)
+
+        def load_rows(dst, src, c):
+            nc.sync.dma_start(out=dst[c][:], in_=src[:, c * CHUNK : (c + 1) * CHUNK, :])
+
+        gain_bf = keep.tile([P, PACK], BF16)
+        shift_bf = keep.tile([P, PACK], BF16)
+        bq_bf = keep.tile([P, PACK], BF16)
+        bo_all = keep.tile([P, D], BF16)
+
+        load_rows(x_sb, x_rows, 0)
+        nc.sync.dma_start(out=gain_bf[:], in_=ln1_g.rearrange("(p t) -> p t", t=PACK))
+        nc.sync.dma_start(out=shift_bf[:], in_=ln1_b.rearrange("(p t) -> p t", t=PACK))
+        load_rows(x_sb, x_rows, 1)
+        load_weight(nc, Wq_words, Wq_scales, wq_words, wq_plane)
+        nc.sync.dma_start(out=bq_bf[:], in_=bq.rearrange("(p t) -> p t", t=PACK))
+        load_rows(x_sb, x_rows, 2)
+        load_rows(x_sb, x_rows, 3)
+        load_rows(yt_sb, yt_rows, 0)
+        nc.sync.dma_start(out=bo_all[:], in_=bo.partition_broadcast(P))
+        load_weight(nc, Wo_words, Wo_scales, wo_words, wo_plane)
+        for c in range(1, CHUNKS):
+            load_rows(yt_sb, yt_rows, c)
+
+        identity = keep.tile([P, P], F32)
+        make_identity(nc, identity[:])
+        minus_half = keep.tile([P, CHUNK], F32)
+        nc.gpsimd.memset(minus_half[:], -0.5)
+
+        warm = keep.tile([P, 1], F32)
+        nc.vector.memset(warm[:], 0.0)
+        nc.scalar.activation(out=warm[:], in_=warm[:], func=ACT.Sigmoid)
+
+        gain = keep.tile([P, PACK], F32)
+        shift = keep.tile([P, PACK], F32)
+        bq_col = keep.tile([P, PACK], F32)
+        nc.vector.tensor_copy(out=gain[:], in_=gain_bf[:])
+        nc.vector.tensor_copy(out=shift[:], in_=shift_bf[:])
+        nc.vector.tensor_copy(out=bq_col[:], in_=bq_bf[:])
+
+        for c in range(CHUNKS):
+            stats = norm.tile([P, CHUNK, 6], F32)
+            mean_var = norm.tile([P, CHUNK, 2], F32)
+            for i in range(CHUNK):
+                nc.vector.bn_stats(out=stats[:, i, :], in_=x_sb[c][:, i, :])
+                nc.vector.bn_aggr(out=mean_var[:, i, :], in_=stats[:, i, :])
+            var_eps = norm.tile([P, CHUNK], F32)
+            rstd = norm.tile([P, CHUNK], F32)
+            minus_mean_rstd = norm.tile([P, CHUNK], F32)
+            nc.gpsimd.tensor_scalar(
+                out=var_eps[:], in0=mean_var[:, :, 1], scalar1=1.0, scalar2=EPS, op0=ALU.mult, op1=ALU.add
+            )
+            nc.gpsimd.tensor_tensor(out=rstd[:], in0=var_eps[:], in1=minus_half[:], op=ALU.pow)
+            nc.vector.scalar_tensor_tensor(
+                out=minus_mean_rstd[:], in0=mean_var[:, :, 0], scalar=-1.0, in1=rstd[:], op0=ALU.mult, op1=ALU.mult
+            )
+
+            x_hat = norm.tile([P, CHUNK, PACK, P], F32)
+            for i in range(CHUNK):
+                nc.scalar.activation(
+                    out=x_hat[:, i, :, :],
+                    in_=x_sb[c][:, i, :].rearrange("r (p t) -> r t p", t=PACK),
+                    func=ACT.Identity,
+                    scale=rstd[:, i : i + 1],
+                    bias=minus_mean_rstd[:, i : i + 1],
+                )
+
+            h_planes = norm.tile([P, PACK, CHUNK_ROWS], BF16)
+            for t in range(PACK):
+                x_hat_t = psum.tile([P, CHUNK_ROWS], F32, tag="transposed")
+                for i in range(CHUNK):
+                    nc.tensor.transpose(x_hat_t[:, i * P : (i + 1) * P], x_hat[:, i, t, :], identity[:])
+                nc.scalar.activation(
+                    out=h_planes[:, t, :],
+                    in_=x_hat_t[:],
+                    func=ACT.Identity,
+                    scale=gain[:, t : t + 1],
+                    bias=shift[:, t : t + 1],
+                )
+            h_grouped = norm.tile([P, CHUNK_ROWS, PACK], BF16, align_bytes=64)
+            nc.vector.tensor_copy(
+                out=h_grouped[:].rearrange("p (c i) t -> p c t i", i=4),
+                in_=h_planes[:].rearrange("p t (c i) -> p c t i", i=4),
+            )
+            h_words = norm.tile([P, CHUNK_ROWS], U32, align_bytes=64)
+            h_plane = norm.tile([P, CHUNK_ROWS], U8, align_bytes=64)
+            nc.vector.quantize_mx(
+                out=h_words[:].bitcast(FP8X4), scales=h_plane[:], in_=h_grouped[:].rearrange("p r t -> p (r t)")
+            )
+
+            q_sorted = gate.tile([P, CHUNK, PACK, P], F32)
+            for i in range(CHUNK):
+                q_bank = psum.tile([P, D], F32, tag="q")
+                nc.tensor.matmul_mx(
+                    out=q_bank[:],
+                    lhsT=h_words[:, i * P : (i + 1) * P].bitcast(FP8X4),
+                    lhsT_scale=h_plane[:, i * P : (i + 1) * P],
+                    rhs=wq_words[:].bitcast(FP8X4),
+                    rhs_scale=wq_plane[:],
+                    start=True,
+                    stop=True,
+                )
+                nc.scalar.copy(out=q_sorted[:, i, :, :], in_=q_bank[:].rearrange("r (p t) -> r t p", t=PACK))
+
+            sig_planes = gate.tile([P, PACK, CHUNK_ROWS], F32)
+            for t in range(PACK):
+                q_t = psum.tile([P, CHUNK_ROWS], F32, tag="transposed")
+                for i in range(CHUNK):
+                    nc.tensor.transpose(q_t[:, i * P : (i + 1) * P], q_sorted[:, i, t, :], identity[:])
+                nc.scalar.activation(
+                    out=sig_planes[:, t, :], in_=q_t[:], func=ACT.Sigmoid, bias=bq_col[:, t : t + 1]
+                )
+
+            y_grouped = gate.tile([P, CHUNK_ROWS, PACK], BF16, align_bytes=64)
+            for half in range(2):
+                yt_t = psum.tile([P, 2, 2, P], F32, tag="yt")
+                for u in range(2):
+                    for j in range(2):
+                        yt_words = yt_sb[c][:, 2 * half + j, :].bitcast(F32).rearrange("r (p u) -> r u p", u=2)
+                        nc.tensor.transpose(yt_t[:, u, j, :], yt_words[:, u, :], identity[:])
+                rows = slice(half * HALF_ROWS, (half + 1) * HALF_ROWS)
+                nc.vector.tensor_tensor(
+                    out=y_grouped[:, rows, :].rearrange("p r (u e) -> p r u e", e=2),
+                    in0=sig_planes[:, :, rows].rearrange("p (u e) r -> p r u e", e=2),
+                    in1=yt_t[:].rearrange("p u j r -> p (u j r)").bitcast(BF16).rearrange(
+                        "p (u r e) -> p r u e", u=2, e=2
+                    ),
+                    op=ALU.mult,
+                )
+            y_words = gate.tile([P, CHUNK_ROWS], U32, align_bytes=64)
+            y_plane = gate.tile([P, CHUNK_ROWS], U8, align_bytes=64)
+            nc.vector.quantize_mx(
+                out=y_words[:].bitcast(FP8X4), scales=y_plane[:], in_=y_grouped[:].rearrange("p r t -> p (r t)")
+            )
+
+            for i in range(CHUNK):
+                x_bo = gate.tile([P, D], F32, bufs=8)
+                nc.gpsimd.tensor_tensor(out=x_bo[:], in0=x_sb[c][:, i, :], in1=bo_all[:], op=ALU.add)
+                o_bank = psum.tile([P, D], F32, tag="o")
+                nc.tensor.matmul_mx(
+                    out=o_bank[:],
+                    lhsT=y_words[:, i * P : (i + 1) * P].bitcast(FP8X4),
+                    lhsT_scale=y_plane[:, i * P : (i + 1) * P],
+                    rhs=wo_words[:].bitcast(FP8X4),
+                    rhs_scale=wo_plane[:],
+                    start=True,
+                    stop=True,
+                )
+                o_sb = gate.tile([P, D], F32, bufs=4)
+                nc.vector.tensor_tensor(out=o_sb[:], in0=o_bank[:], in1=x_bo[:], op=ALU.add)
+                nc.sync.dma_start(out=out_rows[:, c * CHUNK + i, :], in_=o_sb[:])

@@ -51,7 +51,8 @@ def tile_attentionfreetransformerencoder_pb_kernel(
         keep = ctx.enter_context(tc.tile_pool(name="keep", bufs=1))
         norm = ctx.enter_context(tc.tile_pool(name="norm", bufs=CHUNKS))
         gate = ctx.enter_context(tc.tile_pool(name="gate", bufs=2))
-        psum = ctx.enter_context(tc.psum_pool(name="psum", bufs=2))
+        psum = ctx.enter_context(tc.psum_pool(name="psum", bufs=8))
+        ctx.enter_context(tc.manual_schedule())
 
         wq_plane = keep.tile([P, D], U8, align_bytes=64)
         wo_plane = keep.tile([P, D], U8, align_bytes=64)
@@ -62,11 +63,14 @@ def tile_attentionfreetransformerencoder_pb_kernel(
 
         x_sb = []
         yt_sb = []
+        x_bo = []
         for c in range(CHUNKS):
             x_chunk = keep.tile([P, CHUNK, D], BF16, name="x%d" % c)
             x_sb.append(x_chunk)
             yt_chunk = keep.tile([P, CHUNK, D], BF16, name="yt%d" % c)
             yt_sb.append(yt_chunk)
+            x_bo_chunk = keep.tile([P, CHUNK, D], F32, name="x_bo%d" % c)
+            x_bo.append(x_bo_chunk)
 
         def load_rows(dst, src, c):
             nc.sync.dma_start(out=dst[c][:], in_=src[:, c * CHUNK : (c + 1) * CHUNK, :])
@@ -77,15 +81,15 @@ def tile_attentionfreetransformerencoder_pb_kernel(
         bo_all = keep.tile([P, D], BF16)
 
         load_rows(x_sb, x_rows, 0)
+        load_rows(x_sb, x_rows, 1)
         nc.sync.dma_start(out=gain_bf[:], in_=ln1_g.rearrange("(p t) -> p t", t=PACK))
         nc.sync.dma_start(out=shift_bf[:], in_=ln1_b.rearrange("(p t) -> p t", t=PACK))
-        load_rows(x_sb, x_rows, 1)
+        nc.sync.dma_start(out=bo_all[:], in_=bo.partition_broadcast(P))
         load_weight(nc, Wq_words, Wq_scales, wq_words, wq_plane)
         nc.sync.dma_start(out=bq_bf[:], in_=bq.rearrange("(p t) -> p t", t=PACK))
         load_rows(x_sb, x_rows, 2)
         load_rows(x_sb, x_rows, 3)
         load_rows(yt_sb, yt_rows, 0)
-        nc.sync.dma_start(out=bo_all[:], in_=bo.partition_broadcast(P))
         load_weight(nc, Wo_words, Wo_scales, wo_words, wo_plane)
         for c in range(1, CHUNKS):
             load_rows(yt_sb, yt_rows, c)
@@ -99,52 +103,72 @@ def tile_attentionfreetransformerencoder_pb_kernel(
         nc.vector.memset(warm[:], 0.0)
         nc.scalar.activation(out=warm[:], in_=warm[:], func=ACT.Sigmoid)
 
-        gain = keep.tile([P, PACK], F32)
-        shift = keep.tile([P, PACK], F32)
-        bq_col = keep.tile([P, PACK], F32)
-        nc.vector.tensor_copy(out=gain[:], in_=gain_bf[:])
-        nc.vector.tensor_copy(out=shift[:], in_=shift_bf[:])
-        nc.vector.tensor_copy(out=bq_col[:], in_=bq_bf[:])
+        rstd_of = {}
+        bias_of = {}
+        x_hat_of = {}
+        h_words_of = {}
+        h_plane_of = {}
+        q_sorted_of = {}
+        sig_planes_of = {}
+        yt_t_of = {}
+        y_words_of = {}
+        y_plane_of = {}
 
-        for c in range(CHUNKS):
-            stats = norm.tile([P, CHUNK, 6], F32)
+        def stats(c):
+            moments = norm.tile([P, CHUNK, 6], F32)
             mean_var = norm.tile([P, CHUNK, 2], F32)
             for i in range(CHUNK):
-                nc.vector.bn_stats(out=stats[:, i, :], in_=x_sb[c][:, i, :])
-                nc.vector.bn_aggr(out=mean_var[:, i, :], in_=stats[:, i, :])
+                nc.vector.bn_stats(out=moments[:, i, :], in_=x_sb[c][:, i, :])
+            for i in range(CHUNK):
+                nc.vector.bn_aggr(out=mean_var[:, i, :], in_=moments[:, i, :])
+            minus_mean = norm.tile([P, CHUNK], F32)
+            nc.vector.tensor_scalar(
+                out=minus_mean[:], in0=mean_var[:, :, 0], scalar1=-1.0, scalar2=None, op0=ALU.mult
+            )
             var_eps = norm.tile([P, CHUNK], F32)
             rstd = norm.tile([P, CHUNK], F32)
-            minus_mean_rstd = norm.tile([P, CHUNK], F32)
+            bias = norm.tile([P, CHUNK], F32)
             nc.gpsimd.tensor_scalar(
                 out=var_eps[:], in0=mean_var[:, :, 1], scalar1=1.0, scalar2=EPS, op0=ALU.mult, op1=ALU.add
             )
             nc.gpsimd.tensor_tensor(out=rstd[:], in0=var_eps[:], in1=minus_half[:], op=ALU.pow)
-            nc.vector.scalar_tensor_tensor(
-                out=minus_mean_rstd[:], in0=mean_var[:, :, 0], scalar=-1.0, in1=rstd[:], op0=ALU.mult, op1=ALU.mult
-            )
+            nc.gpsimd.tensor_tensor(out=bias[:], in0=minus_mean[:], in1=rstd[:], op=ALU.mult)
+            rstd_of[c] = rstd
+            bias_of[c] = bias
 
+        def residual(c):
+            for i in range(CHUNK):
+                nc.gpsimd.tensor_tensor(out=x_bo[c][:, i, :], in0=x_sb[c][:, i, :], in1=bo_all[:], op=ALU.add)
+
+        def normalise(c):
             x_hat = norm.tile([P, CHUNK, PACK, P], F32)
             for i in range(CHUNK):
                 nc.scalar.activation(
                     out=x_hat[:, i, :, :],
                     in_=x_sb[c][:, i, :].rearrange("r (p t) -> r t p", t=PACK),
                     func=ACT.Identity,
-                    scale=rstd[:, i : i + 1],
-                    bias=minus_mean_rstd[:, i : i + 1],
+                    scale=rstd_of[c][:, i : i + 1],
+                    bias=bias_of[c][:, i : i + 1],
                 )
+            x_hat_of[c] = x_hat
 
-            h_planes = norm.tile([P, PACK, CHUNK_ROWS], BF16)
-            for t in range(PACK):
-                x_hat_t = psum.tile([P, CHUNK_ROWS], F32, tag="transposed")
-                for i in range(CHUNK):
-                    nc.tensor.transpose(x_hat_t[:, i * P : (i + 1) * P], x_hat[:, i, t, :], identity[:])
-                nc.scalar.activation(
-                    out=h_planes[:, t, :],
-                    in_=x_hat_t[:],
-                    func=ACT.Identity,
-                    scale=gain[:, t : t + 1],
-                    bias=shift[:, t : t + 1],
-                )
+        def transposed_plane(sorted_rows, t):
+            plane = psum.tile([P, CHUNK_ROWS], F32, tag="bank")
+            for i in range(CHUNK):
+                nc.tensor.transpose(plane[:, i * P : (i + 1) * P], sorted_rows[:, i, t, :], identity[:])
+            return plane
+
+        def h_plane_t(c, t, h_planes):
+            x_hat_t = transposed_plane(x_hat_of[c], t)
+            nc.scalar.activation(
+                out=h_planes[:, t, :],
+                in_=x_hat_t[:],
+                func=ACT.Identity,
+                scale=gain[:, t : t + 1],
+                bias=shift[:, t : t + 1],
+            )
+
+        def h_quantise(c, h_planes):
             h_grouped = norm.tile([P, CHUNK_ROWS, PACK], BF16, align_bytes=64)
             nc.vector.tensor_copy(
                 out=h_grouped[:].rearrange("p (c i) t -> p c t i", i=4),
@@ -155,44 +179,56 @@ def tile_attentionfreetransformerencoder_pb_kernel(
             nc.vector.quantize_mx(
                 out=h_words[:].bitcast(FP8X4), scales=h_plane[:], in_=h_grouped[:].rearrange("p r t -> p (r t)")
             )
+            h_words_of[c] = h_words
+            h_plane_of[c] = h_plane
 
+        def q_rows(c):
             q_sorted = gate.tile([P, CHUNK, PACK, P], F32)
             for i in range(CHUNK):
-                q_bank = psum.tile([P, D], F32, tag="q")
+                q_bank = psum.tile([P, D], F32, tag="bank")
                 nc.tensor.matmul_mx(
                     out=q_bank[:],
-                    lhsT=h_words[:, i * P : (i + 1) * P].bitcast(FP8X4),
-                    lhsT_scale=h_plane[:, i * P : (i + 1) * P],
+                    lhsT=h_words_of[c][:, i * P : (i + 1) * P].bitcast(FP8X4),
+                    lhsT_scale=h_plane_of[c][:, i * P : (i + 1) * P],
                     rhs=wq_words[:].bitcast(FP8X4),
                     rhs_scale=wq_plane[:],
                     start=True,
                     stop=True,
                 )
                 nc.scalar.copy(out=q_sorted[:, i, :, :], in_=q_bank[:].rearrange("r (p t) -> r t p", t=PACK))
+            q_sorted_of[c] = q_sorted
 
+        def sigmoid_planes(c):
             sig_planes = gate.tile([P, PACK, CHUNK_ROWS], F32)
             for t in range(PACK):
-                q_t = psum.tile([P, CHUNK_ROWS], F32, tag="transposed")
-                for i in range(CHUNK):
-                    nc.tensor.transpose(q_t[:, i * P : (i + 1) * P], q_sorted[:, i, t, :], identity[:])
+                q_t = transposed_plane(q_sorted_of[c], t)
                 nc.scalar.activation(
                     out=sig_planes[:, t, :], in_=q_t[:], func=ACT.Sigmoid, bias=bq_col[:, t : t + 1]
                 )
+            sig_planes_of[c] = sig_planes
 
-            y_grouped = gate.tile([P, CHUNK_ROWS, PACK], BF16, align_bytes=64)
+        def yt_transposed(c):
+            halves = []
             for half in range(2):
-                yt_t = psum.tile([P, 2, 2, P], F32, tag="yt")
+                yt_t = psum.tile([P, 2, 2, P], F32, tag="bank")
                 for u in range(2):
                     for j in range(2):
                         yt_words = yt_sb[c][:, 2 * half + j, :].bitcast(F32).rearrange("r (p u) -> r u p", u=2)
                         nc.tensor.transpose(yt_t[:, u, j, :], yt_words[:, u, :], identity[:])
+                halves.append(yt_t)
+            yt_t_of[c] = halves
+
+        def y_quantise(c):
+            y_grouped = gate.tile([P, CHUNK_ROWS, PACK], BF16, align_bytes=64)
+            for half in range(2):
                 rows = slice(half * HALF_ROWS, (half + 1) * HALF_ROWS)
                 nc.vector.tensor_tensor(
                     out=y_grouped[:, rows, :].rearrange("p r (u e) -> p r u e", e=2),
-                    in0=sig_planes[:, :, rows].rearrange("p (u e) r -> p r u e", e=2),
-                    in1=yt_t[:].rearrange("p u j r -> p (u j r)").bitcast(BF16).rearrange(
-                        "p (u r e) -> p r u e", u=2, e=2
-                    ),
+                    in0=sig_planes_of[c][:, :, rows].rearrange("p (u e) r -> p r u e", e=2),
+                    in1=yt_t_of[c][half][:]
+                    .rearrange("p u j r -> p (u j r)")
+                    .bitcast(BF16)
+                    .rearrange("p (u r e) -> p r u e", u=2, e=2),
                     op=ALU.mult,
                 )
             y_words = gate.tile([P, CHUNK_ROWS], U32, align_bytes=64)
@@ -200,20 +236,55 @@ def tile_attentionfreetransformerencoder_pb_kernel(
             nc.vector.quantize_mx(
                 out=y_words[:].bitcast(FP8X4), scales=y_plane[:], in_=y_grouped[:].rearrange("p r t -> p (r t)")
             )
+            y_words_of[c] = y_words
+            y_plane_of[c] = y_plane
 
-            for i in range(CHUNK):
-                x_bo = gate.tile([P, D], F32, bufs=8)
-                nc.gpsimd.tensor_tensor(out=x_bo[:], in0=x_sb[c][:, i, :], in1=bo_all[:], op=ALU.add)
-                o_bank = psum.tile([P, D], F32, tag="o")
-                nc.tensor.matmul_mx(
-                    out=o_bank[:],
-                    lhsT=y_words[:, i * P : (i + 1) * P].bitcast(FP8X4),
-                    lhsT_scale=y_plane[:, i * P : (i + 1) * P],
-                    rhs=wo_words[:].bitcast(FP8X4),
-                    rhs_scale=wo_plane[:],
-                    start=True,
-                    stop=True,
-                )
-                o_sb = gate.tile([P, D], F32, bufs=4)
-                nc.vector.tensor_tensor(out=o_sb[:], in0=o_bank[:], in1=x_bo[:], op=ALU.add)
-                nc.sync.dma_start(out=out_rows[:, c * CHUNK + i, :], in_=o_sb[:])
+        def project_tile(c, i):
+            o_bank = psum.tile([P, D], F32, tag="bank")
+            nc.tensor.matmul_mx(
+                out=o_bank[:],
+                lhsT=y_words_of[c][:, i * P : (i + 1) * P].bitcast(FP8X4),
+                lhsT_scale=y_plane_of[c][:, i * P : (i + 1) * P],
+                rhs=wo_words[:].bitcast(FP8X4),
+                rhs_scale=wo_plane[:],
+                start=True,
+                stop=True,
+            )
+            o_sb = gate.tile([P, D], F32, bufs=4)
+            nc.vector.tensor_tensor(out=o_sb[:], in0=o_bank[:], in1=x_bo[c][:, i, :], op=ALU.add)
+            nc.sync.dma_start(out=out_rows[:, c * CHUNK + i, :], in_=o_sb[:])
+
+        stats(0)
+        stats(1)
+        gain = keep.tile([P, PACK], F32)
+        shift = keep.tile([P, PACK], F32)
+        bq_col = keep.tile([P, PACK], F32)
+        nc.vector.tensor_copy(out=gain[:], in_=gain_bf[:])
+        nc.vector.tensor_copy(out=shift[:], in_=shift_bf[:])
+        nc.vector.tensor_copy(out=bq_col[:], in_=bq_bf[:])
+
+        for r in range(CHUNKS + 2):
+            norming = r < CHUNKS
+            gating = 0 <= r - 1 < CHUNKS
+            projecting = 0 <= r - 2
+            if projecting:
+                y_quantise(r - 2)
+            if norming:
+                normalise(r)
+                residual(r)
+            if gating:
+                q_rows(r - 1)
+            if r + 2 < CHUNKS:
+                stats(r + 2)
+            if norming:
+                h_planes = norm.tile([P, PACK, CHUNK_ROWS], BF16)
+            for j in range(4):
+                if norming:
+                    h_plane_t(r, j, h_planes)
+                if projecting:
+                    project_tile(r - 2, j)
+            if gating:
+                sigmoid_planes(r - 1)
+                yt_transposed(r - 1)
+            if norming:
+                h_quantise(r, h_planes)

@@ -21,6 +21,7 @@ CHUNK = 4
 CHUNKS = TILES // CHUNK
 CHUNK_ROWS = CHUNK * P
 HALF_ROWS = CHUNK_ROWS // 2
+HALVES = (slice(0, HALF_ROWS), slice(HALF_ROWS, CHUNK_ROWS))
 EPS = 1e-5
 
 FLOPS = 2 * 2 * ROWS * D * D
@@ -104,7 +105,7 @@ def tile_attentionfreetransformerencoder_pb_kernel(
         nc.scalar.activation(out=warm[:], in_=warm[:], func=ACT.Sigmoid)
 
         rstd_of = {}
-        bias_of = {}
+        minus_mean_of = {}
         x_hat_of = {}
         h_words_of = {}
         h_plane_of = {}
@@ -127,14 +128,12 @@ def tile_attentionfreetransformerencoder_pb_kernel(
             )
             var_eps = norm.tile([P, CHUNK], F32)
             rstd = norm.tile([P, CHUNK], F32)
-            bias = norm.tile([P, CHUNK], F32)
             nc.gpsimd.tensor_scalar(
                 out=var_eps[:], in0=mean_var[:, :, 1], scalar1=1.0, scalar2=EPS, op0=ALU.mult, op1=ALU.add
             )
             nc.gpsimd.tensor_tensor(out=rstd[:], in0=var_eps[:], in1=minus_half[:], op=ALU.pow)
-            nc.gpsimd.tensor_tensor(out=bias[:], in0=minus_mean[:], in1=rstd[:], op=ALU.mult)
             rstd_of[c] = rstd
-            bias_of[c] = bias
+            minus_mean_of[c] = minus_mean
 
         def residual(c):
             for i in range(CHUNK):
@@ -143,12 +142,13 @@ def tile_attentionfreetransformerencoder_pb_kernel(
         def normalise(c):
             x_hat = norm.tile([P, CHUNK, PACK, P], F32)
             for i in range(CHUNK):
-                nc.scalar.activation(
+                nc.gpsimd.tensor_scalar(
                     out=x_hat[:, i, :, :],
-                    in_=x_sb[c][:, i, :].rearrange("r (p t) -> r t p", t=PACK),
-                    func=ACT.Identity,
-                    scale=rstd_of[c][:, i : i + 1],
-                    bias=bias_of[c][:, i : i + 1],
+                    in0=x_sb[c][:, i, :].rearrange("r (p t) -> r t p", t=PACK),
+                    scalar1=minus_mean_of[c][:, i : i + 1],
+                    scalar2=rstd_of[c][:, i : i + 1],
+                    op0=ALU.add,
+                    op1=ALU.mult,
                 )
             x_hat_of[c] = x_hat
 
@@ -170,15 +170,19 @@ def tile_attentionfreetransformerencoder_pb_kernel(
 
         def h_quantise(c, h_planes):
             h_grouped = norm.tile([P, CHUNK_ROWS, PACK], BF16, align_bytes=64)
-            nc.vector.tensor_copy(
-                out=h_grouped[:].rearrange("p (c i) t -> p c t i", i=4),
-                in_=h_planes[:].rearrange("p t (c i) -> p c t i", i=4),
-            )
             h_words = norm.tile([P, CHUNK_ROWS], U32, align_bytes=64)
             h_plane = norm.tile([P, CHUNK_ROWS], U8, align_bytes=64)
-            nc.vector.quantize_mx(
-                out=h_words[:].bitcast(FP8X4), scales=h_plane[:], in_=h_grouped[:].rearrange("p r t -> p (r t)")
-            )
+            for rows in HALVES:
+                nc.vector.tensor_copy(
+                    out=h_grouped[:, rows, :].rearrange("p (c i) t -> p c t i", i=4),
+                    in_=h_planes[:, :, rows].rearrange("p t (c i) -> p c t i", i=4),
+                )
+            for rows in HALVES:
+                nc.vector.quantize_mx(
+                    out=h_words[:, rows].bitcast(FP8X4),
+                    scales=h_plane[:, rows],
+                    in_=h_grouped[:, rows, :].rearrange("p r t -> p (r t)"),
+                )
             h_words_of[c] = h_words
             h_plane_of[c] = h_plane
 
@@ -221,7 +225,7 @@ def tile_attentionfreetransformerencoder_pb_kernel(
         def y_quantise(c):
             y_grouped = gate.tile([P, CHUNK_ROWS, PACK], BF16, align_bytes=64)
             for half in range(2):
-                rows = slice(half * HALF_ROWS, (half + 1) * HALF_ROWS)
+                rows = HALVES[half]
                 nc.vector.tensor_tensor(
                     out=y_grouped[:, rows, :].rearrange("p r (u e) -> p r u e", e=2),
                     in0=sig_planes_of[c][:, :, rows].rearrange("p (u e) r -> p r u e", e=2),
@@ -233,9 +237,12 @@ def tile_attentionfreetransformerencoder_pb_kernel(
                 )
             y_words = gate.tile([P, CHUNK_ROWS], U32, align_bytes=64)
             y_plane = gate.tile([P, CHUNK_ROWS], U8, align_bytes=64)
-            nc.vector.quantize_mx(
-                out=y_words[:].bitcast(FP8X4), scales=y_plane[:], in_=y_grouped[:].rearrange("p r t -> p (r t)")
-            )
+            for rows in HALVES:
+                nc.vector.quantize_mx(
+                    out=y_words[:, rows].bitcast(FP8X4),
+                    scales=y_plane[:, rows],
+                    in_=y_grouped[:, rows, :].rearrange("p r t -> p (r t)"),
+                )
             y_words_of[c] = y_words
             y_plane_of[c] = y_plane
 
@@ -255,7 +262,9 @@ def tile_attentionfreetransformerencoder_pb_kernel(
             nc.sync.dma_start(out=out_rows[:, c * CHUNK + i, :], in_=o_sb[:])
 
         stats(0)
+        normalise(0)
         stats(1)
+        normalise(1)
         gain = keep.tile([P, PACK], F32)
         shift = keep.tile([P, PACK], F32)
         bq_col = keep.tile([P, PACK], F32)
@@ -270,19 +279,19 @@ def tile_attentionfreetransformerencoder_pb_kernel(
             if projecting:
                 y_quantise(r - 2)
             if norming:
-                normalise(r)
                 residual(r)
             if gating:
                 q_rows(r - 1)
             if r + 2 < CHUNKS:
                 stats(r + 2)
+                normalise(r + 2)
             if norming:
                 h_planes = norm.tile([P, PACK, CHUNK_ROWS], BF16)
-            for j in range(4):
-                if norming:
-                    h_plane_t(r, j, h_planes)
-                if projecting:
-                    project_tile(r - 2, j)
+                for t in range(PACK):
+                    h_plane_t(r, t, h_planes)
+            if projecting:
+                for i in range(CHUNK):
+                    project_tile(r - 2, i)
             if gating:
                 sigmoid_planes(r - 1)
                 yt_transposed(r - 1)

@@ -81,15 +81,13 @@ def tile_attentionfreetransformerencoder_pb_kernel(
         bq_bf = keep.tile([P, PACK], BF16)
         bo_all = keep.tile([P, D], BF16)
 
-        load_rows(x_sb, x_rows, 0)
-        load_rows(x_sb, x_rows, 1)
+        for c in range(CHUNKS):
+            load_rows(x_sb, x_rows, c)
         nc.sync.dma_start(out=gain_bf[:], in_=ln1_g.rearrange("(p t) -> p t", t=PACK))
         nc.sync.dma_start(out=shift_bf[:], in_=ln1_b.rearrange("(p t) -> p t", t=PACK))
-        nc.sync.dma_start(out=bo_all[:], in_=bo.partition_broadcast(P))
         load_weight(nc, Wq_words, Wq_scales, wq_words, wq_plane)
         nc.sync.dma_start(out=bq_bf[:], in_=bq.rearrange("(p t) -> p t", t=PACK))
-        load_rows(x_sb, x_rows, 2)
-        load_rows(x_sb, x_rows, 3)
+        nc.sync.dma_start(out=bo_all[:], in_=bo.partition_broadcast(P))
         load_rows(yt_sb, yt_rows, 0)
         load_weight(nc, Wo_words, Wo_scales, wo_words, wo_plane)
         for c in range(1, CHUNKS):
@@ -109,7 +107,6 @@ def tile_attentionfreetransformerencoder_pb_kernel(
         x_hat_of = {}
         h_words_of = {}
         h_plane_of = {}
-        q_sorted_of = {}
         sig_planes_of = {}
         yt_t_of = {}
         y_words_of = {}
@@ -186,41 +183,42 @@ def tile_attentionfreetransformerencoder_pb_kernel(
             h_words_of[c] = h_words
             h_plane_of[c] = h_plane
 
-        def q_rows(c):
-            q_sorted = gate.tile([P, CHUNK, PACK, P], F32)
-            for i in range(CHUNK):
-                q_bank = psum.tile([P, D], F32, tag="bank")
-                nc.tensor.matmul_mx(
-                    out=q_bank[:],
-                    lhsT=h_words_of[c][:, i * P : (i + 1) * P].bitcast(FP8X4),
-                    lhsT_scale=h_plane_of[c][:, i * P : (i + 1) * P],
-                    rhs=wq_words[:].bitcast(FP8X4),
-                    rhs_scale=wq_plane[:],
-                    start=True,
-                    stop=True,
-                )
-                nc.scalar.copy(out=q_sorted[:, i, :, :], in_=q_bank[:].rearrange("r (p t) -> r t p", t=PACK))
-            q_sorted_of[c] = q_sorted
+        def q_row_tile(c, i, q_sorted):
+            q_bank = psum.tile([P, D], F32, tag="bank")
+            nc.tensor.matmul_mx(
+                out=q_bank[:],
+                lhsT=h_words_of[c][:, i * P : (i + 1) * P].bitcast(FP8X4),
+                lhsT_scale=h_plane_of[c][:, i * P : (i + 1) * P],
+                rhs=wq_words[:].bitcast(FP8X4),
+                rhs_scale=wq_plane[:],
+                start=True,
+                stop=True,
+            )
+            nc.scalar.copy(out=q_sorted[:, i, :, :], in_=q_bank[:].rearrange("r (p t) -> r t p", t=PACK))
 
-        def sigmoid_planes(c):
-            sig_planes = gate.tile([P, PACK, CHUNK_ROWS], F32)
-            for t in range(PACK):
-                q_t = transposed_plane(q_sorted_of[c], t)
-                nc.scalar.activation(
-                    out=sig_planes[:, t, :], in_=q_t[:], func=ACT.Sigmoid, bias=bq_col[:, t : t + 1]
-                )
-            sig_planes_of[c] = sig_planes
+        def clock_pass():
+            unread = psum.tile([P, D], F32, tag="bank")
+            nc.tensor.matmul_mx(
+                out=unread[:],
+                lhsT=wq_words[:, 0 : P * PACK].bitcast(FP8X4),
+                lhsT_scale=wq_plane[:, 0:P],
+                rhs=wq_words[:].bitcast(FP8X4),
+                rhs_scale=wq_plane[:],
+                start=True,
+                stop=True,
+            )
 
-        def yt_transposed(c):
-            halves = []
-            for half in range(2):
-                yt_t = psum.tile([P, 2, 2, P], F32, tag="bank")
-                for u in range(2):
-                    for j in range(2):
-                        yt_words = yt_sb[c][:, 2 * half + j, :].bitcast(F32).rearrange("r (p u) -> r u p", u=2)
-                        nc.tensor.transpose(yt_t[:, u, j, :], yt_words[:, u, :], identity[:])
-                halves.append(yt_t)
-            yt_t_of[c] = halves
+        def sigmoid_plane_t(t, q_sorted, sig_planes):
+            q_t = transposed_plane(q_sorted, t)
+            nc.scalar.activation(out=sig_planes[:, t, :], in_=q_t[:], func=ACT.Sigmoid, bias=bq_col[:, t : t + 1])
+
+        def yt_transposed(c, half):
+            yt_t = psum.tile([P, 2, 2, P], F32, tag="bank")
+            for u in range(2):
+                for j in range(2):
+                    yt_words = yt_sb[c][:, 2 * half + j, :].bitcast(F32).rearrange("r (p u) -> r u p", u=2)
+                    nc.tensor.transpose(yt_t[:, u, j, :], yt_words[:, u, :], identity[:])
+            yt_t_of[(c, half)] = yt_t
 
         def y_quantise(c):
             y_grouped = gate.tile([P, CHUNK_ROWS, PACK], BF16, align_bytes=64)
@@ -229,7 +227,7 @@ def tile_attentionfreetransformerencoder_pb_kernel(
                 nc.vector.tensor_tensor(
                     out=y_grouped[:, rows, :].rearrange("p r (u e) -> p r u e", e=2),
                     in0=sig_planes_of[c][:, :, rows].rearrange("p (u e) r -> p r u e", e=2),
-                    in1=yt_t_of[c][half][:]
+                    in1=yt_t_of[(c, half)][:]
                     .rearrange("p u j r -> p (u j r)")
                     .bitcast(BF16)
                     .rearrange("p (u r e) -> p r u e", u=2, e=2),
@@ -280,20 +278,30 @@ def tile_attentionfreetransformerencoder_pb_kernel(
                 y_quantise(r - 2)
             if norming:
                 residual(r)
+                h_planes = norm.tile([P, PACK, CHUNK_ROWS], BF16)
             if gating:
-                q_rows(r - 1)
+                q_sorted = gate.tile([P, CHUNK, PACK, P], F32)
+                sig_planes = gate.tile([P, PACK, CHUNK_ROWS], F32)
+                sig_planes_of[r - 1] = sig_planes
+            for pair in ((0, 1), (2, 3)):
+                if gating:
+                    for i in pair:
+                        q_row_tile(r - 1, i, q_sorted)
+                    clock_pass()
+                if norming:
+                    for t in pair:
+                        h_plane_t(r, t, h_planes)
             if r + 2 < CHUNKS:
                 stats(r + 2)
                 normalise(r + 2)
             if norming:
-                h_planes = norm.tile([P, PACK, CHUNK_ROWS], BF16)
-                for t in range(PACK):
-                    h_plane_t(r, t, h_planes)
-            if projecting:
-                for i in range(CHUNK):
-                    project_tile(r - 2, i)
-            if gating:
-                sigmoid_planes(r - 1)
-                yt_transposed(r - 1)
-            if norming:
                 h_quantise(r, h_planes)
+            for pair in ((0, 1), (2, 3)):
+                if projecting:
+                    for i in pair:
+                        project_tile(r - 2, i)
+                    clock_pass()
+                if gating:
+                    for t in pair:
+                        sigmoid_plane_t(t, q_sorted, sig_planes)
+                    yt_transposed(r - 1, pair[0] // 2)

@@ -81,13 +81,15 @@ def tile_attentionfreetransformerencoder_pb_kernel(
         bq_bf = keep.tile([P, PACK], BF16)
         bo_all = keep.tile([P, D], BF16)
 
-        for c in range(CHUNKS):
-            load_rows(x_sb, x_rows, c)
+        load_rows(x_sb, x_rows, 0)
+        load_rows(x_sb, x_rows, 1)
         nc.sync.dma_start(out=gain_bf[:], in_=ln1_g.rearrange("(p t) -> p t", t=PACK))
         nc.sync.dma_start(out=shift_bf[:], in_=ln1_b.rearrange("(p t) -> p t", t=PACK))
+        nc.sync.dma_start(out=bo_all[:], in_=bo.partition_broadcast(P))
         load_weight(nc, Wq_words, Wq_scales, wq_words, wq_plane)
         nc.sync.dma_start(out=bq_bf[:], in_=bq.rearrange("(p t) -> p t", t=PACK))
-        nc.sync.dma_start(out=bo_all[:], in_=bo.partition_broadcast(P))
+        load_rows(x_sb, x_rows, 2)
+        load_rows(x_sb, x_rows, 3)
         load_rows(yt_sb, yt_rows, 0)
         load_weight(nc, Wo_words, Wo_scales, wo_words, wo_plane)
         for c in range(1, CHUNKS):
@@ -105,8 +107,10 @@ def tile_attentionfreetransformerencoder_pb_kernel(
         rstd_of = {}
         minus_mean_of = {}
         x_hat_of = {}
+        h_grouped_of = {}
         h_words_of = {}
         h_plane_of = {}
+        q_sorted_of = {}
         sig_planes_of = {}
         yt_t_of = {}
         y_words_of = {}
@@ -165,60 +169,62 @@ def tile_attentionfreetransformerencoder_pb_kernel(
                 bias=shift[:, t : t + 1],
             )
 
-        def h_quantise(c, h_planes):
+        def h_regroup(c, h_planes):
             h_grouped = norm.tile([P, CHUNK_ROWS, PACK], BF16, align_bytes=64)
-            h_words = norm.tile([P, CHUNK_ROWS], U32, align_bytes=64)
-            h_plane = norm.tile([P, CHUNK_ROWS], U8, align_bytes=64)
             for rows in HALVES:
-                nc.vector.tensor_copy(
+                nc.scalar.copy(
                     out=h_grouped[:, rows, :].rearrange("p (c i) t -> p c t i", i=4),
                     in_=h_planes[:, :, rows].rearrange("p t (c i) -> p c t i", i=4),
                 )
+            h_grouped_of[c] = h_grouped
+
+        def h_quantise(c):
+            h_words = norm.tile([P, CHUNK_ROWS], U32, align_bytes=64)
+            h_plane = norm.tile([P, CHUNK_ROWS], U8, align_bytes=64)
             for rows in HALVES:
                 nc.vector.quantize_mx(
                     out=h_words[:, rows].bitcast(FP8X4),
                     scales=h_plane[:, rows],
-                    in_=h_grouped[:, rows, :].rearrange("p r t -> p (r t)"),
+                    in_=h_grouped_of[c][:, rows, :].rearrange("p r t -> p (r t)"),
                 )
             h_words_of[c] = h_words
             h_plane_of[c] = h_plane
 
-        def q_row_tile(c, i, q_sorted):
-            q_bank = psum.tile([P, D], F32, tag="bank")
-            nc.tensor.matmul_mx(
-                out=q_bank[:],
-                lhsT=h_words_of[c][:, i * P : (i + 1) * P].bitcast(FP8X4),
-                lhsT_scale=h_plane_of[c][:, i * P : (i + 1) * P],
-                rhs=wq_words[:].bitcast(FP8X4),
-                rhs_scale=wq_plane[:],
-                start=True,
-                stop=True,
-            )
-            nc.scalar.copy(out=q_sorted[:, i, :, :], in_=q_bank[:].rearrange("r (p t) -> r t p", t=PACK))
+        def q_rows(c):
+            q_sorted = gate.tile([P, CHUNK, PACK, P], F32)
+            for i in range(CHUNK):
+                q_bank = psum.tile([P, D], F32, tag="bank")
+                nc.tensor.matmul_mx(
+                    out=q_bank[:],
+                    lhsT=h_words_of[c][:, i * P : (i + 1) * P].bitcast(FP8X4),
+                    lhsT_scale=h_plane_of[c][:, i * P : (i + 1) * P],
+                    rhs=wq_words[:].bitcast(FP8X4),
+                    rhs_scale=wq_plane[:],
+                    start=True,
+                    stop=True,
+                )
+                nc.scalar.copy(out=q_sorted[:, i, :, :], in_=q_bank[:].rearrange("r (p t) -> r t p", t=PACK))
+            q_sorted_of[c] = q_sorted
 
-        def clock_pass():
-            unread = psum.tile([P, D], F32, tag="bank")
-            nc.tensor.matmul_mx(
-                out=unread[:],
-                lhsT=wq_words[:, 0 : P * PACK].bitcast(FP8X4),
-                lhsT_scale=wq_plane[:, 0:P],
-                rhs=wq_words[:].bitcast(FP8X4),
-                rhs_scale=wq_plane[:],
-                start=True,
-                stop=True,
-            )
+        def sigmoid_planes(c):
+            sig_planes = gate.tile([P, PACK, CHUNK_ROWS], F32)
+            for t in range(PACK):
+                q_t = transposed_plane(q_sorted_of[c], t)
+                nc.scalar.activation(
+                    out=sig_planes[:, t, :], in_=q_t[:], func=ACT.Sigmoid, bias=bq_col[:, t : t + 1]
+                )
+            sig_planes_of[c] = sig_planes
 
-        def sigmoid_plane_t(t, q_sorted, sig_planes):
-            q_t = transposed_plane(q_sorted, t)
-            nc.scalar.activation(out=sig_planes[:, t, :], in_=q_t[:], func=ACT.Sigmoid, bias=bq_col[:, t : t + 1])
-
-        def yt_transposed(c, half):
-            yt_t = psum.tile([P, 2, 2, P], F32, tag="bank")
-            for u in range(2):
-                for j in range(2):
-                    yt_words = yt_sb[c][:, 2 * half + j, :].bitcast(F32).rearrange("r (p u) -> r u p", u=2)
-                    nc.tensor.transpose(yt_t[:, u, j, :], yt_words[:, u, :], identity[:])
-            yt_t_of[(c, half)] = yt_t
+        def yt_transposed(c):
+            halves = []
+            for half in range(2):
+                yt_t = psum.tile([P, 2, 2, P], F32, tag="bank")
+                for u in range(2):
+                    for j in range(2):
+                        yt_words = yt_sb[c][:, 2 * half + j, :].bitcast(F32).rearrange("r (p u) -> r u p", u=2)
+                        nc.tensor.transpose(yt_t[:, u, j, :], yt_words[:, u, :], identity[:])
+                halves.append(yt_t)
+            yt_t_of[c] = halves
 
         def y_quantise(c):
             y_grouped = gate.tile([P, CHUNK_ROWS, PACK], BF16, align_bytes=64)
@@ -227,7 +233,7 @@ def tile_attentionfreetransformerencoder_pb_kernel(
                 nc.vector.tensor_tensor(
                     out=y_grouped[:, rows, :].rearrange("p r (u e) -> p r u e", e=2),
                     in0=sig_planes_of[c][:, :, rows].rearrange("p (u e) r -> p r u e", e=2),
-                    in1=yt_t_of[(c, half)][:]
+                    in1=yt_t_of[c][half][:]
                     .rearrange("p u j r -> p (u j r)")
                     .bitcast(BF16)
                     .rearrange("p (u r e) -> p r u e", u=2, e=2),
@@ -278,30 +284,21 @@ def tile_attentionfreetransformerencoder_pb_kernel(
                 y_quantise(r - 2)
             if norming:
                 residual(r)
-                h_planes = norm.tile([P, PACK, CHUNK_ROWS], BF16)
             if gating:
-                q_sorted = gate.tile([P, CHUNK, PACK, P], F32)
-                sig_planes = gate.tile([P, PACK, CHUNK_ROWS], F32)
-                sig_planes_of[r - 1] = sig_planes
-            for pair in ((0, 1), (2, 3)):
-                if gating:
-                    for i in pair:
-                        q_row_tile(r - 1, i, q_sorted)
-                    clock_pass()
-                if norming:
-                    for t in pair:
-                        h_plane_t(r, t, h_planes)
+                q_rows(r - 1)
             if r + 2 < CHUNKS:
                 stats(r + 2)
                 normalise(r + 2)
             if norming:
-                h_quantise(r, h_planes)
-            for pair in ((0, 1), (2, 3)):
-                if projecting:
-                    for i in pair:
-                        project_tile(r - 2, i)
-                    clock_pass()
-                if gating:
-                    for t in pair:
-                        sigmoid_plane_t(t, q_sorted, sig_planes)
-                    yt_transposed(r - 1, pair[0] // 2)
+                h_planes = norm.tile([P, PACK, CHUNK_ROWS], BF16)
+                for t in range(PACK):
+                    h_plane_t(r, t, h_planes)
+                h_regroup(r, h_planes)
+            if projecting:
+                for i in range(CHUNK):
+                    project_tile(r - 2, i)
+            if norming:
+                h_quantise(r)
+            if gating:
+                sigmoid_planes(r - 1)
+                yt_transposed(r - 1)

@@ -20,19 +20,25 @@ TILES = ROWS // P
 CHUNK = 4
 CHUNKS = TILES // CHUNK
 CHUNK_ROWS = CHUNK * P
-HALF_ROWS = CHUNK_ROWS // 2
-HALVES = (slice(0, HALF_ROWS), slice(HALF_ROWS, CHUNK_ROWS))
+HALVES = (slice(0, CHUNK_ROWS // 2), slice(CHUNK_ROWS // 2, CHUNK_ROWS))
+PSUM_BANKS = 8
+QUADRANT = 32
+QUADRANTS = P // QUADRANT
+SCALE_ROWS = 4
+BN_STATS_DIM = 6
+BN_AGGR_DIM = 2
+RUN = 4
 EPS = 1e-5
 
 FLOPS = 2 * 2 * ROWS * D * D
 
 
-def load_weight(nc, words_dram, scales_dram, words, plane):
-    scale_rows = scales_dram.rearrange("g q n -> (g q) n")
-    for quadrant in range(4):
+def load_weight(nc, words_dram, scales_dram, words, scales):
+    scale_rows = scales_dram.rearrange("g b n -> (g b) n")
+    for quadrant in range(QUADRANTS):
         nc.sync.dma_start(
-            out=plane[32 * quadrant : 32 * quadrant + 4, :].bitcast(I32),
-            in_=scale_rows[4 * quadrant : 4 * quadrant + 4, :].bitcast(I32),
+            out=scales[QUADRANT * quadrant : QUADRANT * quadrant + SCALE_ROWS, :].bitcast(I32),
+            in_=scale_rows[SCALE_ROWS * quadrant : SCALE_ROWS * (quadrant + 1), :].bitcast(I32),
         )
     nc.sync.dma_start(
         out=words[:].bitcast(I32),
@@ -52,13 +58,13 @@ def tile_attentionfreetransformerencoder_pb_kernel(
         keep = ctx.enter_context(tc.tile_pool(name="keep", bufs=1))
         norm = ctx.enter_context(tc.tile_pool(name="norm", bufs=CHUNKS))
         gate = ctx.enter_context(tc.tile_pool(name="gate", bufs=2))
-        psum = ctx.enter_context(tc.psum_pool(name="psum", bufs=8))
+        psum = ctx.enter_context(tc.psum_pool(name="psum", bufs=PSUM_BANKS))
         ctx.enter_context(tc.manual_schedule())
 
-        wq_plane = keep.tile([P, D], U8, align_bytes=64)
-        wo_plane = keep.tile([P, D], U8, align_bytes=64)
-        nc.vector.memset(wq_plane[:].bitcast(I32), 0)
-        nc.vector.memset(wo_plane[:].bitcast(I32), 0)
+        wq_scales = keep.tile([P, D], U8, align_bytes=64)
+        wo_scales = keep.tile([P, D], U8, align_bytes=64)
+        nc.vector.memset(wq_scales[:].bitcast(I32), 0)
+        nc.vector.memset(wo_scales[:].bitcast(I32), 0)
         wq_words = keep.tile([P, D * PACK], U8, align_bytes=64)
         wo_words = keep.tile([P, D * PACK], U8, align_bytes=64)
 
@@ -81,17 +87,15 @@ def tile_attentionfreetransformerencoder_pb_kernel(
         bq_bf = keep.tile([P, PACK], BF16)
         bo_all = keep.tile([P, D], BF16)
 
-        load_rows(x_sb, x_rows, 0)
-        load_rows(x_sb, x_rows, 1)
+        for c in range(CHUNKS):
+            load_rows(x_sb, x_rows, c)
         nc.sync.dma_start(out=gain_bf[:], in_=ln1_g.rearrange("(p t) -> p t", t=PACK))
         nc.sync.dma_start(out=shift_bf[:], in_=ln1_b.rearrange("(p t) -> p t", t=PACK))
-        nc.sync.dma_start(out=bo_all[:], in_=bo.partition_broadcast(P))
-        load_weight(nc, Wq_words, Wq_scales, wq_words, wq_plane)
+        load_weight(nc, Wq_words, Wq_scales, wq_words, wq_scales)
         nc.sync.dma_start(out=bq_bf[:], in_=bq.rearrange("(p t) -> p t", t=PACK))
-        load_rows(x_sb, x_rows, 2)
-        load_rows(x_sb, x_rows, 3)
+        nc.sync.dma_start(out=bo_all[:], in_=bo.partition_broadcast(P))
         load_rows(yt_sb, yt_rows, 0)
-        load_weight(nc, Wo_words, Wo_scales, wo_words, wo_plane)
+        load_weight(nc, Wo_words, Wo_scales, wo_words, wo_scales)
         for c in range(1, CHUNKS):
             load_rows(yt_sb, yt_rows, c)
 
@@ -104,21 +108,21 @@ def tile_attentionfreetransformerencoder_pb_kernel(
         nc.vector.memset(warm[:], 0.0)
         nc.scalar.activation(out=warm[:], in_=warm[:], func=ACT.Sigmoid)
 
-        rstd_of = {}
         minus_mean_of = {}
+        rstd_of = {}
         x_hat_of = {}
         h_grouped_of = {}
         h_words_of = {}
-        h_plane_of = {}
+        h_scales_of = {}
         q_sorted_of = {}
-        sig_planes_of = {}
+        sig_by_t_of = {}
         yt_t_of = {}
         y_words_of = {}
-        y_plane_of = {}
+        y_scales_of = {}
 
         def stats(c):
-            moments = norm.tile([P, CHUNK, 6], F32)
-            mean_var = norm.tile([P, CHUNK, 2], F32)
+            moments = norm.tile([P, CHUNK, BN_STATS_DIM], F32)
+            mean_var = norm.tile([P, CHUNK, BN_AGGR_DIM], F32)
             for i in range(CHUNK):
                 nc.vector.bn_stats(out=moments[:, i, :], in_=x_sb[c][:, i, :])
             for i in range(CHUNK):
@@ -133,12 +137,8 @@ def tile_attentionfreetransformerencoder_pb_kernel(
                 out=var_eps[:], in0=mean_var[:, :, 1], scalar1=1.0, scalar2=EPS, op0=ALU.mult, op1=ALU.add
             )
             nc.gpsimd.tensor_tensor(out=rstd[:], in0=var_eps[:], in1=minus_half[:], op=ALU.pow)
-            rstd_of[c] = rstd
             minus_mean_of[c] = minus_mean
-
-        def residual(c):
-            for i in range(CHUNK):
-                nc.gpsimd.tensor_tensor(out=x_bo[c][:, i, :], in0=x_sb[c][:, i, :], in1=bo_all[:], op=ALU.add)
+            rstd_of[c] = rstd
 
         def normalise(c):
             x_hat = norm.tile([P, CHUNK, PACK, P], F32)
@@ -153,86 +153,90 @@ def tile_attentionfreetransformerencoder_pb_kernel(
                 )
             x_hat_of[c] = x_hat
 
-        def transposed_plane(sorted_rows, t):
-            plane = psum.tile([P, CHUNK_ROWS], F32, tag="bank")
+        def residual(c):
             for i in range(CHUNK):
-                nc.tensor.transpose(plane[:, i * P : (i + 1) * P], sorted_rows[:, i, t, :], identity[:])
-            return plane
+                nc.gpsimd.tensor_tensor(out=x_bo[c][:, i, :], in0=x_sb[c][:, i, :], in1=bo_all[:], op=ALU.add)
 
-        def h_plane_t(c, t, h_planes):
-            x_hat_t = transposed_plane(x_hat_of[c], t)
-            nc.scalar.activation(
-                out=h_planes[:, t, :],
-                in_=x_hat_t[:],
-                func=ACT.Identity,
-                scale=gain[:, t : t + 1],
-                bias=shift[:, t : t + 1],
-            )
+        def transposed(sorted_rows, t):
+            bank = psum.tile([P, CHUNK_ROWS], F32, tag="bank")
+            for i in range(CHUNK):
+                nc.tensor.transpose(bank[:, i * P : (i + 1) * P], sorted_rows[:, i, t, :], identity[:])
+            return bank
 
-        def h_regroup(c, h_planes):
-            h_grouped = norm.tile([P, CHUNK_ROWS, PACK], BF16, align_bytes=64)
-            for rows in HALVES:
-                nc.scalar.copy(
-                    out=h_grouped[:, rows, :].rearrange("p (c i) t -> p c t i", i=4),
-                    in_=h_planes[:, :, rows].rearrange("p t (c i) -> p c t i", i=4),
-                )
-            h_grouped_of[c] = h_grouped
-
-        def h_quantise(c):
-            h_words = norm.tile([P, CHUNK_ROWS], U32, align_bytes=64)
-            h_plane = norm.tile([P, CHUNK_ROWS], U8, align_bytes=64)
+        def quantise(grouped, words, scales):
             for rows in HALVES:
                 nc.vector.quantize_mx(
-                    out=h_words[:, rows].bitcast(FP8X4),
-                    scales=h_plane[:, rows],
-                    in_=h_grouped_of[c][:, rows, :].rearrange("p r t -> p (r t)"),
+                    out=words[:, rows].bitcast(FP8X4),
+                    scales=scales[:, rows],
+                    in_=grouped[:, rows, :].rearrange("p r t -> p (r t)"),
                 )
-            h_words_of[c] = h_words
-            h_plane_of[c] = h_plane
 
-        def q_rows(c):
-            q_sorted = gate.tile([P, CHUNK, PACK, P], F32)
+        def h_grouped(c):
+            h_by_t = norm.tile([P, PACK, CHUNK_ROWS], BF16)
+            for t in range(PACK):
+                x_hat_t = transposed(x_hat_of[c], t)
+                nc.scalar.activation(
+                    out=h_by_t[:, t, :],
+                    in_=x_hat_t[:],
+                    func=ACT.Identity,
+                    scale=gain[:, t : t + 1],
+                    bias=shift[:, t : t + 1],
+                )
+            grouped = norm.tile([P, CHUNK_ROWS, PACK], BF16, align_bytes=64)
+            nc.scalar.copy(
+                out=grouped[:].rearrange("p (c i) t -> p c t i", i=RUN),
+                in_=h_by_t[:].rearrange("p t (c i) -> p c t i", i=RUN),
+            )
+            h_grouped_of[c] = grouped
+
+        def h_quantised(c):
+            h_words = norm.tile([P, CHUNK_ROWS], U32, align_bytes=64)
+            h_scales = norm.tile([P, CHUNK_ROWS], U8, align_bytes=64)
+            quantise(h_grouped_of[c], h_words, h_scales)
+            h_words_of[c] = h_words
+            h_scales_of[c] = h_scales
+
+        def q_sorted(c):
+            sorted_rows = gate.tile([P, CHUNK, PACK, P], F32)
             for i in range(CHUNK):
                 q_bank = psum.tile([P, D], F32, tag="bank")
                 nc.tensor.matmul_mx(
                     out=q_bank[:],
                     lhsT=h_words_of[c][:, i * P : (i + 1) * P].bitcast(FP8X4),
-                    lhsT_scale=h_plane_of[c][:, i * P : (i + 1) * P],
+                    lhsT_scale=h_scales_of[c][:, i * P : (i + 1) * P],
                     rhs=wq_words[:].bitcast(FP8X4),
-                    rhs_scale=wq_plane[:],
+                    rhs_scale=wq_scales[:],
                     start=True,
                     stop=True,
                 )
-                nc.scalar.copy(out=q_sorted[:, i, :, :], in_=q_bank[:].rearrange("r (p t) -> r t p", t=PACK))
-            q_sorted_of[c] = q_sorted
+                nc.scalar.copy(out=sorted_rows[:, i, :, :], in_=q_bank[:].rearrange("r (p t) -> r t p", t=PACK))
+            q_sorted_of[c] = sorted_rows
 
-        def sigmoid_planes(c):
-            sig_planes = gate.tile([P, PACK, CHUNK_ROWS], F32)
+        def sigmoid_by_t(c):
+            sig_by_t = gate.tile([P, PACK, CHUNK_ROWS], F32)
             for t in range(PACK):
-                q_t = transposed_plane(q_sorted_of[c], t)
-                nc.scalar.activation(
-                    out=sig_planes[:, t, :], in_=q_t[:], func=ACT.Sigmoid, bias=bq_col[:, t : t + 1]
-                )
-            sig_planes_of[c] = sig_planes
+                q_t = transposed(q_sorted_of[c], t)
+                nc.scalar.activation(out=sig_by_t[:, t, :], in_=q_t[:], func=ACT.Sigmoid, bias=bq_col[:, t : t + 1])
+            sig_by_t_of[c] = sig_by_t
 
         def yt_transposed(c):
-            halves = []
+            banks = []
             for half in range(2):
                 yt_t = psum.tile([P, 2, 2, P], F32, tag="bank")
                 for u in range(2):
                     for j in range(2):
                         yt_words = yt_sb[c][:, 2 * half + j, :].bitcast(F32).rearrange("r (p u) -> r u p", u=2)
                         nc.tensor.transpose(yt_t[:, u, j, :], yt_words[:, u, :], identity[:])
-                halves.append(yt_t)
-            yt_t_of[c] = halves
+                banks.append(yt_t)
+            yt_t_of[c] = banks
 
-        def y_quantise(c):
-            y_grouped = gate.tile([P, CHUNK_ROWS, PACK], BF16, align_bytes=64)
+        def y_quantised(c):
+            grouped = gate.tile([P, CHUNK_ROWS, PACK], BF16, align_bytes=64)
             for half in range(2):
                 rows = HALVES[half]
                 nc.vector.tensor_tensor(
-                    out=y_grouped[:, rows, :].rearrange("p r (u e) -> p r u e", e=2),
-                    in0=sig_planes_of[c][:, :, rows].rearrange("p (u e) r -> p r u e", e=2),
+                    out=grouped[:, rows, :].rearrange("p r (u e) -> p r u e", e=2),
+                    in0=sig_by_t_of[c][:, :, rows].rearrange("p (u e) r -> p r u e", e=2),
                     in1=yt_t_of[c][half][:]
                     .rearrange("p u j r -> p (u j r)")
                     .bitcast(BF16)
@@ -240,35 +244,30 @@ def tile_attentionfreetransformerencoder_pb_kernel(
                     op=ALU.mult,
                 )
             y_words = gate.tile([P, CHUNK_ROWS], U32, align_bytes=64)
-            y_plane = gate.tile([P, CHUNK_ROWS], U8, align_bytes=64)
-            for rows in HALVES:
-                nc.vector.quantize_mx(
-                    out=y_words[:, rows].bitcast(FP8X4),
-                    scales=y_plane[:, rows],
-                    in_=y_grouped[:, rows, :].rearrange("p r t -> p (r t)"),
-                )
+            y_scales = gate.tile([P, CHUNK_ROWS], U8, align_bytes=64)
+            quantise(grouped, y_words, y_scales)
             y_words_of[c] = y_words
-            y_plane_of[c] = y_plane
+            y_scales_of[c] = y_scales
 
-        def project_tile(c, i):
-            o_bank = psum.tile([P, D], F32, tag="bank")
-            nc.tensor.matmul_mx(
-                out=o_bank[:],
-                lhsT=y_words_of[c][:, i * P : (i + 1) * P].bitcast(FP8X4),
-                lhsT_scale=y_plane_of[c][:, i * P : (i + 1) * P],
-                rhs=wo_words[:].bitcast(FP8X4),
-                rhs_scale=wo_plane[:],
-                start=True,
-                stop=True,
-            )
-            o_sb = gate.tile([P, D], F32, bufs=4)
-            nc.vector.tensor_tensor(out=o_sb[:], in0=o_bank[:], in1=x_bo[c][:, i, :], op=ALU.add)
-            nc.sync.dma_start(out=out_rows[:, c * CHUNK + i, :], in_=o_sb[:])
+        def projected(c):
+            for i in range(CHUNK):
+                o_bank = psum.tile([P, D], F32, tag="bank")
+                nc.tensor.matmul_mx(
+                    out=o_bank[:],
+                    lhsT=y_words_of[c][:, i * P : (i + 1) * P].bitcast(FP8X4),
+                    lhsT_scale=y_scales_of[c][:, i * P : (i + 1) * P],
+                    rhs=wo_words[:].bitcast(FP8X4),
+                    rhs_scale=wo_scales[:],
+                    start=True,
+                    stop=True,
+                )
+                o_sb = gate.tile([P, D], F32, bufs=CHUNK)
+                nc.vector.tensor_tensor(out=o_sb[:], in0=o_bank[:], in1=x_bo[c][:, i, :], op=ALU.add)
+                nc.sync.dma_start(out=out_rows[:, c * CHUNK + i, :], in_=o_sb[:])
 
-        stats(0)
-        normalise(0)
-        stats(1)
-        normalise(1)
+        for c in range(2):
+            stats(c)
+            normalise(c)
         gain = keep.tile([P, PACK], F32)
         shift = keep.tile([P, PACK], F32)
         bq_col = keep.tile([P, PACK], F32)
@@ -281,24 +280,20 @@ def tile_attentionfreetransformerencoder_pb_kernel(
             gating = 0 <= r - 1 < CHUNKS
             projecting = 0 <= r - 2
             if projecting:
-                y_quantise(r - 2)
+                y_quantised(r - 2)
             if norming:
                 residual(r)
             if gating:
-                q_rows(r - 1)
+                q_sorted(r - 1)
             if r + 2 < CHUNKS:
                 stats(r + 2)
                 normalise(r + 2)
             if norming:
-                h_planes = norm.tile([P, PACK, CHUNK_ROWS], BF16)
-                for t in range(PACK):
-                    h_plane_t(r, t, h_planes)
-                h_regroup(r, h_planes)
+                h_grouped(r)
             if projecting:
-                for i in range(CHUNK):
-                    project_tile(r - 2, i)
+                projected(r - 2)
             if norming:
-                h_quantise(r)
+                h_quantised(r)
             if gating:
-                sigmoid_planes(r - 1)
+                sigmoid_by_t(r - 1)
                 yt_transposed(r - 1)

@@ -17,10 +17,9 @@ D = 512
 PACK = 4
 ROWS = 2048
 TILES = ROWS // P
-CHUNK = 4
-CHUNKS = TILES // CHUNK
-CHUNK_ROWS = CHUNK * P
-HALVES = (slice(0, CHUNK_ROWS // 2), slice(CHUNK_ROWS // 2, CHUNK_ROWS))
+UNIT = 2
+UNITS = TILES // UNIT
+UNIT_ROWS = UNIT * P
 PSUM_BANKS = 8
 QUADRANT = 32
 QUADRANTS = P // QUADRANT
@@ -29,6 +28,8 @@ BN_STATS_DIM = 6
 BN_AGGR_DIM = 2
 RUN = 4
 EPS = 1e-5
+STATS_LEAD = 3
+NORM_LEAD = 2
 
 FLOPS = 2 * 2 * ROWS * D * D
 
@@ -56,8 +57,8 @@ def tile_attentionfreetransformerencoder_pb_kernel(
 
     with ExitStack() as ctx:
         keep = ctx.enter_context(tc.tile_pool(name="keep", bufs=1))
-        norm = ctx.enter_context(tc.tile_pool(name="norm", bufs=CHUNKS))
-        gate = ctx.enter_context(tc.tile_pool(name="gate", bufs=2))
+        small = ctx.enter_context(tc.tile_pool(name="small", bufs=UNITS))
+        work = ctx.enter_context(tc.tile_pool(name="work", bufs=4))
         psum = ctx.enter_context(tc.psum_pool(name="psum", bufs=PSUM_BANKS))
         ctx.enter_context(tc.manual_schedule())
 
@@ -67,233 +68,269 @@ def tile_attentionfreetransformerencoder_pb_kernel(
         nc.vector.memset(wo_scales[:].bitcast(I32), 0)
         wq_words = keep.tile([P, D * PACK], U8, align_bytes=64)
         wo_words = keep.tile([P, D * PACK], U8, align_bytes=64)
+        wq_perm_words = keep.tile([P, D], I32, align_bytes=64)
+        wq_perm_scales = keep.tile([P, D], U8, align_bytes=64)
 
         x_sb = []
         yt_sb = []
         x_bo = []
-        for c in range(CHUNKS):
-            x_chunk = keep.tile([P, CHUNK, D], BF16, name="x%d" % c)
-            x_sb.append(x_chunk)
-            yt_chunk = keep.tile([P, CHUNK, D], BF16, name="yt%d" % c)
-            yt_sb.append(yt_chunk)
-            x_bo_chunk = keep.tile([P, CHUNK, D], F32, name="x_bo%d" % c)
-            x_bo.append(x_bo_chunk)
+        for u in range(UNITS):
+            x_unit = keep.tile([P, UNIT, D], BF16, name="x%d" % u)
+            x_sb.append(x_unit)
+            yt_unit = keep.tile([P, UNIT, D], BF16, name="yt%d" % u)
+            yt_sb.append(yt_unit)
+            x_bo_unit = keep.tile([P, UNIT, D], F32, name="x_bo%d" % u)
+            x_bo.append(x_bo_unit)
 
-        def load_rows(dst, src, c):
-            nc.sync.dma_start(out=dst[c][:], in_=src[:, c * CHUNK : (c + 1) * CHUNK, :])
+        def load_rows(dst, src, u):
+            nc.sync.dma_start(out=dst[u][:], in_=src[:, u * UNIT : (u + 1) * UNIT, :])
 
         gain_bf = keep.tile([P, PACK], BF16)
         shift_bf = keep.tile([P, PACK], BF16)
         bq_bf = keep.tile([P, PACK], BF16)
         bo_all = keep.tile([P, D], BF16)
 
-        for c in range(CHUNKS):
-            load_rows(x_sb, x_rows, c)
+        for u in range(3):
+            load_rows(x_sb, x_rows, u)
         nc.sync.dma_start(out=gain_bf[:], in_=ln1_g.rearrange("(p t) -> p t", t=PACK))
         nc.sync.dma_start(out=shift_bf[:], in_=ln1_b.rearrange("(p t) -> p t", t=PACK))
         load_weight(nc, Wq_words, Wq_scales, wq_words, wq_scales)
         nc.sync.dma_start(out=bq_bf[:], in_=bq.rearrange("(p t) -> p t", t=PACK))
-        nc.sync.dma_start(out=bo_all[:], in_=bo.partition_broadcast(P))
+        for u in range(3, 5):
+            load_rows(x_sb, x_rows, u)
         load_rows(yt_sb, yt_rows, 0)
+        nc.sync.dma_start(out=bo_all[:], in_=bo.partition_broadcast(P))
         load_weight(nc, Wo_words, Wo_scales, wo_words, wo_scales)
-        for c in range(1, CHUNKS):
-            load_rows(yt_sb, yt_rows, c)
+        for u in range(5, UNITS):
+            load_rows(x_sb, x_rows, u)
+            load_rows(yt_sb, yt_rows, u - 4)
+        for u in range(UNITS - 4, UNITS):
+            load_rows(yt_sb, yt_rows, u)
 
         identity = keep.tile([P, P], F32)
         make_identity(nc, identity[:])
-        minus_half = keep.tile([P, CHUNK], F32)
+        minus_half = keep.tile([P, UNIT], F32)
         nc.gpsimd.memset(minus_half[:], -0.5)
 
         warm = keep.tile([P, 1], F32)
         nc.vector.memset(warm[:], 0.0)
         nc.scalar.activation(out=warm[:], in_=warm[:], func=ACT.Sigmoid)
 
-        minus_mean_of = {}
+        gain = keep.tile([P, PACK], F32)
+        shift = keep.tile([P, PACK], F32)
+        bq_col = keep.tile([P, PACK], F32)
+
+        mean_var_of = {}
         rstd_of = {}
         x_hat_of = {}
+        x_hat_t_of = {}
+        h_by_t_of = {}
         h_grouped_of = {}
         h_words_of = {}
         h_scales_of = {}
-        q_sorted_of = {}
+        q_t_of = {}
         sig_by_t_of = {}
         yt_t_of = {}
+        y_grouped_of = {}
         y_words_of = {}
         y_scales_of = {}
+        o_bank_of = {}
 
-        def stats(c):
-            moments = norm.tile([P, CHUNK, BN_STATS_DIM], F32)
-            mean_var = norm.tile([P, CHUNK, BN_AGGR_DIM], F32)
-            for i in range(CHUNK):
-                nc.vector.bn_stats(out=moments[:, i, :], in_=x_sb[c][:, i, :])
-            for i in range(CHUNK):
+        def stats(u):
+            moments = small.tile([P, UNIT, BN_STATS_DIM], F32)
+            mean_var = small.tile([P, UNIT, BN_AGGR_DIM], F32)
+            for i in range(UNIT):
+                nc.vector.bn_stats(out=moments[:, i, :], in_=x_sb[u][:, i, :])
+            for i in range(UNIT):
                 nc.vector.bn_aggr(out=mean_var[:, i, :], in_=moments[:, i, :])
-            minus_mean = norm.tile([P, CHUNK], F32)
-            nc.vector.tensor_scalar(
-                out=minus_mean[:], in0=mean_var[:, :, 0], scalar1=-1.0, scalar2=None, op0=ALU.mult
-            )
-            var_eps = norm.tile([P, CHUNK], F32)
-            rstd = norm.tile([P, CHUNK], F32)
-            nc.gpsimd.tensor_scalar(
-                out=var_eps[:], in0=mean_var[:, :, 1], scalar1=1.0, scalar2=EPS, op0=ALU.mult, op1=ALU.add
-            )
+            var_eps = small.tile([P, UNIT], F32)
+            rstd = small.tile([P, UNIT], F32)
+            nc.vector.tensor_scalar(out=var_eps[:], in0=mean_var[:, :, 1], scalar1=EPS, scalar2=None, op0=ALU.add)
             nc.gpsimd.tensor_tensor(out=rstd[:], in0=var_eps[:], in1=minus_half[:], op=ALU.pow)
-            minus_mean_of[c] = minus_mean
-            rstd_of[c] = rstd
+            mean_var_of[u] = mean_var
+            rstd_of[u] = rstd
 
-        def normalise(c):
-            x_hat = norm.tile([P, CHUNK, PACK, P], F32)
-            for i in range(CHUNK):
+        def normalise(u):
+            x_hat = work.tile([P, UNIT, PACK, P], F32)
+            for i in range(UNIT):
                 nc.gpsimd.tensor_scalar(
                     out=x_hat[:, i, :, :],
-                    in0=x_sb[c][:, i, :].rearrange("r (p t) -> r t p", t=PACK),
-                    scalar1=minus_mean_of[c][:, i : i + 1],
-                    scalar2=rstd_of[c][:, i : i + 1],
-                    op0=ALU.add,
+                    in0=x_sb[u][:, i, :].rearrange("r (p t) -> r t p", t=PACK),
+                    scalar1=mean_var_of[u][:, i, 0:1],
+                    scalar2=rstd_of[u][:, i : i + 1],
+                    op0=ALU.subtract,
                     op1=ALU.mult,
                 )
-            x_hat_of[c] = x_hat
+            x_hat_of[u] = x_hat
 
-        def residual(c):
-            for i in range(CHUNK):
-                nc.gpsimd.tensor_tensor(out=x_bo[c][:, i, :], in0=x_sb[c][:, i, :], in1=bo_all[:], op=ALU.add)
+        def residual(u):
+            for i in range(UNIT):
+                nc.gpsimd.tensor_tensor(out=x_bo[u][:, i, :], in0=x_sb[u][:, i, :], in1=bo_all[:], op=ALU.add)
 
-        def transposed(sorted_rows, t):
-            bank = psum.tile([P, CHUNK_ROWS], F32, tag="bank")
-            for i in range(CHUNK):
-                nc.tensor.transpose(bank[:, i * P : (i + 1) * P], sorted_rows[:, i, t, :], identity[:])
-            return bank
+        def x_hat_transposed(u):
+            banks = []
+            for pair in range(PACK // 2):
+                bank = psum.tile([P, 2, UNIT_ROWS], F32, tag="bank")
+                for e in range(2):
+                    for i in range(UNIT):
+                        nc.tensor.transpose(
+                            bank[:, e, i * P : (i + 1) * P], x_hat_of[u][:, i, 2 * pair + e, :], identity[:]
+                        )
+                banks.append(bank)
+            x_hat_t_of[u] = banks
 
-        def quantise(grouped, words, scales):
-            for rows in HALVES:
-                nc.vector.quantize_mx(
-                    out=words[:, rows].bitcast(FP8X4),
-                    scales=scales[:, rows],
-                    in_=grouped[:, rows, :].rearrange("p r t -> p (r t)"),
-                )
-
-        def h_grouped(c):
-            h_by_t = norm.tile([P, PACK, CHUNK_ROWS], BF16)
+        def h_by_t(u):
+            by_t = work.tile([P, PACK, UNIT_ROWS], BF16)
             for t in range(PACK):
-                x_hat_t = transposed(x_hat_of[c], t)
                 nc.scalar.activation(
-                    out=h_by_t[:, t, :],
-                    in_=x_hat_t[:],
+                    out=by_t[:, t, :],
+                    in_=x_hat_t_of[u][t // 2][:, t % 2, :],
                     func=ACT.Identity,
                     scale=gain[:, t : t + 1],
                     bias=shift[:, t : t + 1],
                 )
-            grouped = norm.tile([P, CHUNK_ROWS, PACK], BF16, align_bytes=64)
+            h_by_t_of[u] = by_t
+
+        def h_grouped(u):
+            grouped = work.tile([P, UNIT_ROWS, PACK], BF16, align_bytes=64)
             nc.scalar.copy(
                 out=grouped[:].rearrange("p (c i) t -> p c t i", i=RUN),
-                in_=h_by_t[:].rearrange("p t (c i) -> p c t i", i=RUN),
+                in_=h_by_t_of[u][:].rearrange("p t (c i) -> p c t i", i=RUN),
             )
-            h_grouped_of[c] = grouped
+            h_grouped_of[u] = grouped
 
-        def h_quantised(c):
-            h_words = norm.tile([P, CHUNK_ROWS], U32, align_bytes=64)
-            h_scales = norm.tile([P, CHUNK_ROWS], U8, align_bytes=64)
-            quantise(h_grouped_of[c], h_words, h_scales)
-            h_words_of[c] = h_words
-            h_scales_of[c] = h_scales
+        def quantise(grouped, words, scales):
+            nc.vector.quantize_mx(
+                out=words[:].bitcast(FP8X4),
+                scales=scales[:],
+                in_=grouped[:].rearrange("p r t -> p (r t)"),
+            )
 
-        def q_sorted(c):
-            sorted_rows = gate.tile([P, CHUNK, PACK, P], F32)
-            for i in range(CHUNK):
-                q_bank = psum.tile([P, D], F32, tag="bank")
-                nc.tensor.matmul_mx(
-                    out=q_bank[:],
-                    lhsT=h_words_of[c][:, i * P : (i + 1) * P].bitcast(FP8X4),
-                    lhsT_scale=h_scales_of[c][:, i * P : (i + 1) * P],
-                    rhs=wq_words[:].bitcast(FP8X4),
-                    rhs_scale=wq_scales[:],
-                    start=True,
-                    stop=True,
-                )
-                nc.scalar.copy(out=sorted_rows[:, i, :, :], in_=q_bank[:].rearrange("r (p t) -> r t p", t=PACK))
-            q_sorted_of[c] = sorted_rows
+        def h_quantised(u):
+            h_words = work.tile([P, UNIT_ROWS], U32, align_bytes=64)
+            h_scales = work.tile([P, UNIT_ROWS], U8, align_bytes=64)
+            quantise(h_grouped_of[u], h_words, h_scales)
+            h_words_of[u] = h_words
+            h_scales_of[u] = h_scales
 
-        def sigmoid_by_t(c):
-            sig_by_t = gate.tile([P, PACK, CHUNK_ROWS], F32)
-            for t in range(PACK):
-                q_t = transposed(q_sorted_of[c], t)
-                nc.scalar.activation(out=sig_by_t[:, t, :], in_=q_t[:], func=ACT.Sigmoid, bias=bq_col[:, t : t + 1])
-            sig_by_t_of[c] = sig_by_t
-
-        def yt_transposed(c):
+        def q_transposed(u):
             banks = []
-            for half in range(2):
-                yt_t = psum.tile([P, 2, 2, P], F32, tag="bank")
-                for u in range(2):
-                    for j in range(2):
-                        yt_words = yt_sb[c][:, 2 * half + j, :].bitcast(F32).rearrange("r (p u) -> r u p", u=2)
-                        nc.tensor.transpose(yt_t[:, u, j, :], yt_words[:, u, :], identity[:])
-                banks.append(yt_t)
-            yt_t_of[c] = banks
+            for pair in range(PACK // 2):
+                bank = psum.tile([P, 2, UNIT_ROWS], F32, tag="bank")
+                for e in range(2):
+                    t = 2 * pair + e
+                    nc.tensor.matmul_mx(
+                        out=bank[:, e, :],
+                        lhsT=wq_perm_words[:, t * P : (t + 1) * P].bitcast(FP8X4),
+                        lhsT_scale=wq_perm_scales[:, t * P : (t + 1) * P],
+                        rhs=h_words_of[u][:].bitcast(FP8X4),
+                        rhs_scale=h_scales_of[u][:],
+                        start=True,
+                        stop=True,
+                    )
+                banks.append(bank)
+            q_t_of[u] = banks
 
-        def y_quantised(c):
-            grouped = gate.tile([P, CHUNK_ROWS, PACK], BF16, align_bytes=64)
-            for half in range(2):
-                rows = HALVES[half]
-                nc.vector.tensor_tensor(
-                    out=grouped[:, rows, :].rearrange("p r (u e) -> p r u e", e=2),
-                    in0=sig_by_t_of[c][:, :, rows].rearrange("p (u e) r -> p r u e", e=2),
-                    in1=yt_t_of[c][half][:]
-                    .rearrange("p u j r -> p (u j r)")
-                    .bitcast(BF16)
-                    .rearrange("p (u r e) -> p r u e", u=2, e=2),
-                    op=ALU.mult,
+        def sigmoid_by_t(u):
+            sig_by_t = work.tile([P, PACK, UNIT_ROWS], F32)
+            for t in range(PACK):
+                nc.scalar.activation(
+                    out=sig_by_t[:, t, :],
+                    in_=q_t_of[u][t // 2][:, t % 2, :],
+                    func=ACT.Sigmoid,
+                    bias=bq_col[:, t : t + 1],
                 )
-            y_words = gate.tile([P, CHUNK_ROWS], U32, align_bytes=64)
-            y_scales = gate.tile([P, CHUNK_ROWS], U8, align_bytes=64)
-            quantise(grouped, y_words, y_scales)
-            y_words_of[c] = y_words
-            y_scales_of[c] = y_scales
+            sig_by_t_of[u] = sig_by_t
 
-        def projected(c):
-            for i in range(CHUNK):
+        def yt_transposed(u):
+            yt_t = psum.tile([P, 2, UNIT, P], F32, tag="bank")
+            for w in range(2):
+                for i in range(UNIT):
+                    yt_words = yt_sb[u][:, i, :].bitcast(F32).rearrange("r (p w) -> r w p", w=2)
+                    nc.tensor.transpose(yt_t[:, w, i, :], yt_words[:, w, :], identity[:])
+            yt_t_of[u] = yt_t
+
+        def y_grouped(u):
+            grouped = work.tile([P, UNIT_ROWS, PACK], BF16, align_bytes=64, name="y_grouped")
+            nc.vector.tensor_tensor(
+                out=grouped[:].rearrange("p r (w e) -> p r w e", e=2),
+                in0=sig_by_t_of[u][:].rearrange("p (w e) r -> p r w e", e=2),
+                in1=yt_t_of[u][:]
+                .rearrange("p w i r -> p (w i r)")
+                .bitcast(BF16)
+                .rearrange("p (w r e) -> p r w e", w=2, e=2),
+                op=ALU.mult,
+            )
+            y_grouped_of[u] = grouped
+
+        def y_quantised(u):
+            y_words = work.tile([P, UNIT_ROWS], U32, align_bytes=64)
+            y_scales = work.tile([P, UNIT_ROWS], U8, align_bytes=64)
+            quantise(y_grouped_of[u], y_words, y_scales)
+            y_words_of[u] = y_words
+            y_scales_of[u] = y_scales
+
+        def projected(u):
+            banks = []
+            for i in range(UNIT):
                 o_bank = psum.tile([P, D], F32, tag="bank")
                 nc.tensor.matmul_mx(
                     out=o_bank[:],
-                    lhsT=y_words_of[c][:, i * P : (i + 1) * P].bitcast(FP8X4),
-                    lhsT_scale=y_scales_of[c][:, i * P : (i + 1) * P],
+                    lhsT=y_words_of[u][:, i * P : (i + 1) * P].bitcast(FP8X4),
+                    lhsT_scale=y_scales_of[u][:, i * P : (i + 1) * P],
                     rhs=wo_words[:].bitcast(FP8X4),
                     rhs_scale=wo_scales[:],
                     start=True,
                     stop=True,
                 )
-                o_sb = gate.tile([P, D], F32, bufs=CHUNK)
-                nc.vector.tensor_tensor(out=o_sb[:], in0=o_bank[:], in1=x_bo[c][:, i, :], op=ALU.add)
-                nc.sync.dma_start(out=out_rows[:, c * CHUNK + i, :], in_=o_sb[:])
+                banks.append(o_bank)
+            o_bank_of[u] = banks
 
-        for c in range(2):
-            stats(c)
-            normalise(c)
-        gain = keep.tile([P, PACK], F32)
-        shift = keep.tile([P, PACK], F32)
-        bq_col = keep.tile([P, PACK], F32)
-        nc.vector.tensor_copy(out=gain[:], in_=gain_bf[:])
-        nc.vector.tensor_copy(out=shift[:], in_=shift_bf[:])
-        nc.vector.tensor_copy(out=bq_col[:], in_=bq_bf[:])
+        def stored(u):
+            for i in range(UNIT):
+                o_sb = work.tile([P, D], F32)
+                nc.vector.tensor_tensor(out=o_sb[:], in0=o_bank_of[u][i][:], in1=x_bo[u][:, i, :], op=ALU.add)
+                nc.sync.dma_start(out=out_rows[:, u * UNIT + i, :], in_=o_sb[:])
 
-        for r in range(CHUNKS + 2):
-            norming = r < CHUNKS
-            gating = 0 <= r - 1 < CHUNKS
-            projecting = 0 <= r - 2
-            if projecting:
-                y_quantised(r - 2)
-            if norming:
-                residual(r)
-            if gating:
-                q_sorted(r - 1)
-            if r + 2 < CHUNKS:
-                stats(r + 2)
-                normalise(r + 2)
-            if norming:
-                h_grouped(r)
-            if projecting:
-                projected(r - 2)
-            if norming:
-                h_quantised(r)
-            if gating:
-                sigmoid_by_t(r - 1)
-                yt_transposed(r - 1)
+        def constants():
+            nc.vector.tensor_copy(out=gain[:], in_=gain_bf[:])
+            nc.vector.tensor_copy(out=shift[:], in_=shift_bf[:])
+            nc.vector.tensor_copy(out=bq_col[:], in_=bq_bf[:])
+            nc.vector.tensor_copy(
+                out=wq_perm_words[:].rearrange("p (t m) -> p t m", t=PACK),
+                in_=wq_words[:].bitcast(I32).rearrange("p (m t) -> p t m", t=PACK),
+            )
+            nc.vector.tensor_copy(
+                out=wq_perm_scales[:].rearrange("p (t m) -> p m t", t=PACK),
+                in_=wq_scales[:].rearrange("p (m t) -> p m t", t=PACK),
+            )
+
+        def live(u):
+            return 0 <= u < UNITS
+
+        for j in range(-STATS_LEAD, UNITS + 1):
+            if live(j - 1):
+                y_grouped(j - 1)
+            if live(j):
+                h_grouped(j)
+                h_quantised(j)
+                q_transposed(j)
+            if live(j - 1):
+                y_quantised(j - 1)
+                projected(j - 1)
+            if live(j + 1):
+                h_by_t(j + 1)
+            if live(j):
+                sigmoid_by_t(j)
+                yt_transposed(j)
+            if live(j + STATS_LEAD):
+                stats(j + STATS_LEAD)
+            if j == -2:
+                constants()
+            if live(j + NORM_LEAD):
+                normalise(j + NORM_LEAD)
+                x_hat_transposed(j + NORM_LEAD)
+            if live(j):
+                residual(j)
+            if live(j - 1):
+                stored(j - 1)

@@ -120,7 +120,7 @@ def tile_attentionfreetransformerencoder_pb_kernel(
         shift = keep.tile([P, PACK], F32)
         bq_col = keep.tile([P, PACK], F32)
 
-        mean_var_of = {}
+        minus_mean_of = {}
         rstd_of = {}
         x_hat_of = {}
         x_hat_t_of = {}
@@ -146,19 +146,23 @@ def tile_attentionfreetransformerencoder_pb_kernel(
             var_eps = small.tile([P, UNIT], F32)
             rstd = small.tile([P, UNIT], F32)
             nc.vector.tensor_scalar(out=var_eps[:], in0=mean_var[:, :, 1], scalar1=EPS, scalar2=None, op0=ALU.add)
+            minus_mean = small.tile([P, UNIT], F32)
+            nc.vector.tensor_scalar(
+                out=minus_mean[:], in0=mean_var[:, :, 0], scalar1=-1.0, scalar2=None, op0=ALU.mult
+            )
             nc.gpsimd.tensor_tensor(out=rstd[:], in0=var_eps[:], in1=minus_half[:], op=ALU.pow)
-            mean_var_of[u] = mean_var
+            minus_mean_of[u] = minus_mean
             rstd_of[u] = rstd
 
         def normalise(u):
             x_hat = work.tile([P, UNIT, PACK, P], F32)
             for i in range(UNIT):
-                nc.gpsimd.tensor_scalar(
+                nc.vector.tensor_scalar(
                     out=x_hat[:, i, :, :],
                     in0=x_sb[u][:, i, :].rearrange("r (p t) -> r t p", t=PACK),
-                    scalar1=mean_var_of[u][:, i, 0:1],
+                    scalar1=minus_mean_of[u][:, i : i + 1],
                     scalar2=rstd_of[u][:, i : i + 1],
-                    op0=ALU.subtract,
+                    op0=ALU.add,
                     op1=ALU.mult,
                 )
             x_hat_of[u] = x_hat

@@ -30,6 +30,9 @@ RUN = 4
 EPS = 1e-5
 STATS_LEAD = 3
 NORM_LEAD = 2
+WARM_FROM = 0
+WARM_Q = 3
+WARM_X = 3
 
 FLOPS = 2 * 2 * ROWS * D * D
 
@@ -59,7 +62,7 @@ def tile_attentionfreetransformerencoder_pb_kernel(
         keep = ctx.enter_context(tc.tile_pool(name="keep", bufs=1))
         small = ctx.enter_context(tc.tile_pool(name="small", bufs=UNITS))
         work = ctx.enter_context(tc.tile_pool(name="work", bufs=4))
-        psum = ctx.enter_context(tc.psum_pool(name="psum", bufs=PSUM_BANKS))
+        psum = ctx.enter_context(tc.psum_pool(name="psum", bufs=2))
         ctx.enter_context(tc.manual_schedule())
 
         wq_scales = keep.tile([P, D], U8, align_bytes=64)
@@ -145,12 +148,14 @@ def tile_attentionfreetransformerencoder_pb_kernel(
                 nc.vector.bn_aggr(out=mean_var[:, i, :], in_=moments[:, i, :])
             var_eps = small.tile([P, UNIT], F32)
             rstd = small.tile([P, UNIT], F32)
-            nc.vector.tensor_scalar(out=var_eps[:], in0=mean_var[:, :, 1], scalar1=EPS, scalar2=None, op0=ALU.add)
-            minus_mean = small.tile([P, UNIT], F32)
-            nc.vector.tensor_scalar(
-                out=minus_mean[:], in0=mean_var[:, :, 0], scalar1=-1.0, scalar2=None, op0=ALU.mult
+            nc.gpsimd.tensor_scalar(
+                out=var_eps[:], in0=mean_var[:, :, 1], scalar1=1.0, scalar2=EPS, op0=ALU.mult, op1=ALU.add
             )
             nc.gpsimd.tensor_tensor(out=rstd[:], in0=var_eps[:], in1=minus_half[:], op=ALU.pow)
+            minus_mean = small.tile([P, UNIT], F32)
+            nc.gpsimd.tensor_scalar(
+                out=minus_mean[:], in0=mean_var[:, :, 0], scalar1=-1.0, scalar2=0.0, op0=ALU.mult, op1=ALU.add
+            )
             minus_mean_of[u] = minus_mean
             rstd_of[u] = rstd
 
@@ -171,10 +176,24 @@ def tile_attentionfreetransformerencoder_pb_kernel(
             for i in range(UNIT):
                 nc.gpsimd.tensor_tensor(out=x_bo[u][:, i, :], in0=x_sb[u][:, i, :], in1=bo_all[:], op=ALU.add)
 
+        def unread_passes(bank, count):
+            for n in range(count):
+                nc.tensor.matmul_mx(
+                    out=bank[:].rearrange("p e r -> p (e r)"),
+                    lhsT=wq_perm_words[:, 0:P].bitcast(FP8X4),
+                    lhsT_scale=wq_perm_scales[:, 0:P],
+                    rhs=wo_words[:].bitcast(FP8X4),
+                    rhs_scale=wo_scales[:],
+                    start=True,
+                    stop=True,
+                )
+
         def x_hat_transposed(u):
             banks = []
             for pair in range(PACK // 2):
-                bank = psum.tile([P, 2, UNIT_ROWS], F32, tag="bank")
+                bank = psum.tile([P, 2, UNIT_ROWS], F32, tag="x")
+                if pair == 0 and u >= WARM_FROM + NORM_LEAD:
+                    unread_passes(bank, WARM_X)
                 for e in range(2):
                     for i in range(UNIT):
                         nc.tensor.transpose(
@@ -220,7 +239,9 @@ def tile_attentionfreetransformerencoder_pb_kernel(
         def q_transposed(u):
             banks = []
             for pair in range(PACK // 2):
-                bank = psum.tile([P, 2, UNIT_ROWS], F32, tag="bank")
+                bank = psum.tile([P, 2, UNIT_ROWS], F32, tag="q")
+                if pair == 0 and u >= WARM_FROM:
+                    unread_passes(bank, WARM_Q)
                 for e in range(2):
                     t = 2 * pair + e
                     nc.tensor.matmul_mx(
@@ -247,7 +268,7 @@ def tile_attentionfreetransformerencoder_pb_kernel(
             sig_by_t_of[u] = sig_by_t
 
         def yt_transposed(u):
-            yt_t = psum.tile([P, 2, UNIT, P], F32, tag="bank")
+            yt_t = psum.tile([P, 2, UNIT, P], F32, tag="yt")
             for w in range(2):
                 for i in range(UNIT):
                     yt_words = yt_sb[u][:, i, :].bitcast(F32).rearrange("r (p w) -> r w p", w=2)
@@ -277,7 +298,7 @@ def tile_attentionfreetransformerencoder_pb_kernel(
         def projected(u):
             banks = []
             for i in range(UNIT):
-                o_bank = psum.tile([P, D], F32, tag="bank")
+                o_bank = psum.tile([P, D], F32, tag="o")
                 nc.tensor.matmul_mx(
                     out=o_bank[:],
                     lhsT=y_words_of[u][:, i * P : (i + 1) * P].bitcast(FP8X4),
@@ -326,7 +347,6 @@ def tile_attentionfreetransformerencoder_pb_kernel(
                 h_by_t(j + 1)
             if live(j):
                 sigmoid_by_t(j)
-                yt_transposed(j)
             if live(j + STATS_LEAD):
                 stats(j + STATS_LEAD)
             if j == -2:
@@ -334,6 +354,8 @@ def tile_attentionfreetransformerencoder_pb_kernel(
             if live(j + NORM_LEAD):
                 normalise(j + NORM_LEAD)
                 x_hat_transposed(j + NORM_LEAD)
+            if live(j + 1):
+                yt_transposed(j + 1)
             if live(j):
                 residual(j)
             if live(j - 1):

@@ -31,6 +31,7 @@ EPS = 1e-5
 STATS_LEAD = 3
 NORM_LEAD = 2
 WARM_FROM = 0
+NORM_ENGINES = ("vector", "vector")
 WARM_Q = 3
 WARM_X = 3
 
@@ -91,23 +92,29 @@ def tile_attentionfreetransformerencoder_pb_kernel(
         gain_bf = keep.tile([P, PACK], BF16)
         shift_bf = keep.tile([P, PACK], BF16)
         bq_bf = keep.tile([P, PACK], BF16)
-        bo_all = keep.tile([P, D], BF16)
+        bo_all = keep.tile([P, D], F32)
 
-        for u in range(3):
-            load_rows(x_sb, x_rows, u)
+        bo_row = keep.tile([P, D], BF16)
+        nc.gpsimd.memset(bo_row[:], 0.0)
+        ones = keep.tile([P, P], BF16)
+        nc.gpsimd.memset(ones[:], 1.0)
+
+        load_rows(x_sb, x_rows, 0)
+        nc.sync.dma_start(out=bo_row[0:1, :], in_=bo.rearrange("(o n) -> o n", o=1))
+        load_rows(x_sb, x_rows, 1)
         nc.sync.dma_start(out=gain_bf[:], in_=ln1_g.rearrange("(p t) -> p t", t=PACK))
         nc.sync.dma_start(out=shift_bf[:], in_=ln1_b.rearrange("(p t) -> p t", t=PACK))
+        load_rows(x_sb, x_rows, 2)
         load_weight(nc, Wq_words, Wq_scales, wq_words, wq_scales)
         nc.sync.dma_start(out=bq_bf[:], in_=bq.rearrange("(p t) -> p t", t=PACK))
-        for u in range(3, 5):
-            load_rows(x_sb, x_rows, u)
         load_rows(yt_sb, yt_rows, 0)
-        nc.sync.dma_start(out=bo_all[:], in_=bo.partition_broadcast(P))
+        load_rows(x_sb, x_rows, 3)
+        load_rows(yt_sb, yt_rows, 1)
         load_weight(nc, Wo_words, Wo_scales, wo_words, wo_scales)
-        for u in range(5, UNITS):
+        for u in range(4, UNITS):
             load_rows(x_sb, x_rows, u)
-            load_rows(yt_sb, yt_rows, u - 4)
-        for u in range(UNITS - 4, UNITS):
+            load_rows(yt_sb, yt_rows, u - 2)
+        for u in range(UNITS - 2, UNITS):
             load_rows(yt_sb, yt_rows, u)
 
         identity = keep.tile([P, P], F32)
@@ -119,11 +126,16 @@ def tile_attentionfreetransformerencoder_pb_kernel(
         nc.vector.memset(warm[:], 0.0)
         nc.scalar.activation(out=warm[:], in_=warm[:], func=ACT.Sigmoid)
 
+        bo_bank = psum.tile([P, D], F32, tag="o")
+        nc.tensor.matmul(out=bo_bank[:], lhsT=ones[:], rhs=bo_row[:], start=True, stop=True)
+        nc.scalar.copy(out=bo_all[:], in_=bo_bank[:])
+
         gain = keep.tile([P, PACK], F32)
-        shift = keep.tile([P, PACK], F32)
-        bq_col = keep.tile([P, PACK], F32)
+        shift = shift_bf
+        bq_col = bq_bf
 
         minus_mean_of = {}
+        minus_mean_rstd_of = {}
         rstd_of = {}
         x_hat_of = {}
         x_hat_t_of = {}
@@ -157,19 +169,34 @@ def tile_attentionfreetransformerencoder_pb_kernel(
                 out=minus_mean[:], in0=mean_var[:, :, 0], scalar1=-1.0, scalar2=0.0, op0=ALU.mult, op1=ALU.add
             )
             minus_mean_of[u] = minus_mean
+            if "scalar" in NORM_ENGINES:
+                minus_mean_rstd = small.tile([P, UNIT], F32)
+                nc.gpsimd.tensor_tensor(out=minus_mean_rstd[:], in0=minus_mean[:], in1=rstd[:], op=ALU.mult)
+                minus_mean_rstd_of[u] = minus_mean_rstd
             rstd_of[u] = rstd
 
         def normalise(u):
             x_hat = work.tile([P, UNIT, PACK, P], F32)
             for i in range(UNIT):
-                nc.vector.tensor_scalar(
-                    out=x_hat[:, i, :, :],
-                    in0=x_sb[u][:, i, :].rearrange("r (p t) -> r t p", t=PACK),
-                    scalar1=minus_mean_of[u][:, i : i + 1],
-                    scalar2=rstd_of[u][:, i : i + 1],
-                    op0=ALU.add,
-                    op1=ALU.mult,
-                )
+                sorted_x = x_sb[u][:, i, :].rearrange("r (p t) -> r t p", t=PACK)
+                if NORM_ENGINES[i] == "scalar":
+                    nc.scalar.activation(
+                        out=x_hat[:, i, :, :],
+                        in_=sorted_x,
+                        func=ACT.Identity,
+                        scale=rstd_of[u][:, i : i + 1],
+                        bias=minus_mean_rstd_of[u][:, i : i + 1],
+                    )
+                else:
+                    engine = nc.vector if NORM_ENGINES[i] == "vector" else nc.gpsimd
+                    engine.tensor_scalar(
+                        out=x_hat[:, i, :, :],
+                        in0=sorted_x,
+                        scalar1=minus_mean_of[u][:, i : i + 1],
+                        scalar2=rstd_of[u][:, i : i + 1],
+                        op0=ALU.add,
+                        op1=ALU.mult,
+                    )
             x_hat_of[u] = x_hat
 
         def residual(u):
@@ -182,8 +209,8 @@ def tile_attentionfreetransformerencoder_pb_kernel(
                     out=bank[:].rearrange("p e r -> p (e r)"),
                     lhsT=wq_perm_words[:, 0:P].bitcast(FP8X4),
                     lhsT_scale=wq_perm_scales[:, 0:P],
-                    rhs=wo_words[:].bitcast(FP8X4),
-                    rhs_scale=wo_scales[:],
+                    rhs=wq_words[:].bitcast(FP8X4),
+                    rhs_scale=wq_scales[:],
                     start=True,
                     stop=True,
                 )
@@ -319,16 +346,15 @@ def tile_attentionfreetransformerencoder_pb_kernel(
 
         def constants():
             nc.vector.tensor_copy(out=gain[:], in_=gain_bf[:])
-            nc.vector.tensor_copy(out=shift[:], in_=shift_bf[:])
-            nc.vector.tensor_copy(out=bq_col[:], in_=bq_bf[:])
             nc.vector.tensor_copy(
                 out=wq_perm_words[:].rearrange("p (t m) -> p t m", t=PACK),
                 in_=wq_words[:].bitcast(I32).rearrange("p (m t) -> p t m", t=PACK),
             )
-            nc.vector.tensor_copy(
-                out=wq_perm_scales[:].rearrange("p (t m) -> p m t", t=PACK),
-                in_=wq_scales[:].rearrange("p (m t) -> p m t", t=PACK),
-            )
+            for t in range(PACK):
+                nc.vector.tensor_copy(
+                    out=wq_perm_scales[:, t * P : (t + 1) * P],
+                    in_=wq_scales[:].rearrange("p (m t) -> p t m", t=PACK)[:, t, :],
+                )
 
         def live(u):
             return 0 <= u < UNITS

@@ -359,13 +359,15 @@ def tile_attentionfreetransformerencoder_pb_kernel(
         def live(u):
             return 0 <= u < UNITS
 
-        for j in range(-STATS_LEAD, UNITS + 1):
+        for j in range(-STATS_LEAD, UNITS + 2):
             if live(j - 1):
                 y_grouped(j - 1)
             if live(j):
                 h_grouped(j)
                 h_quantised(j)
                 q_transposed(j)
+            if live(j - 2):
+                stored(j - 2)
             if live(j - 1):
                 y_quantised(j - 1)
                 projected(j - 1)
@@ -384,5 +386,3 @@ def tile_attentionfreetransformerencoder_pb_kernel(
                 yt_transposed(j + 1)
             if live(j):
                 residual(j)
-            if live(j - 1):
-                stored(j - 1)

@@ -31,7 +31,15 @@ EPS = 1e-5
 STATS_LEAD = 3
 NORM_LEAD = 2
 WARM_FROM = 0
-NORM_ENGINES = ("vector", "vector")
+
+
+def norm_engine(u, i):
+    return "scalar" if i else "vector"
+
+
+def residual_engine(u, i):
+    return "vector"
+
 WARM_Q = 3
 WARM_X = 3
 
@@ -131,10 +139,12 @@ def tile_attentionfreetransformerencoder_pb_kernel(
         nc.scalar.copy(out=bo_all[:], in_=bo_bank[:])
 
         gain = keep.tile([P, PACK], F32)
+        nc.gpsimd.tensor_copy(out=gain[:], in_=gain_bf[:])
         shift = shift_bf
         bq_col = bq_bf
 
         minus_mean_of = {}
+        mean_var_of = {}
         minus_mean_rstd_of = {}
         rstd_of = {}
         x_hat_of = {}
@@ -156,6 +166,10 @@ def tile_attentionfreetransformerencoder_pb_kernel(
             mean_var = small.tile([P, UNIT, BN_AGGR_DIM], F32)
             for i in range(UNIT):
                 nc.vector.bn_stats(out=moments[:, i, :], in_=x_sb[u][:, i, :])
+            mean_var_of[u] = (moments, mean_var)
+
+        def aggregate(u):
+            moments, mean_var = mean_var_of[u]
             for i in range(UNIT):
                 nc.vector.bn_aggr(out=mean_var[:, i, :], in_=moments[:, i, :])
             var_eps = small.tile([P, UNIT], F32)
@@ -169,7 +183,7 @@ def tile_attentionfreetransformerencoder_pb_kernel(
                 out=minus_mean[:], in0=mean_var[:, :, 0], scalar1=-1.0, scalar2=0.0, op0=ALU.mult, op1=ALU.add
             )
             minus_mean_of[u] = minus_mean
-            if "scalar" in NORM_ENGINES:
+            if "scalar" in [norm_engine(u, i) for i in range(UNIT)]:
                 minus_mean_rstd = small.tile([P, UNIT], F32)
                 nc.gpsimd.tensor_tensor(out=minus_mean_rstd[:], in0=minus_mean[:], in1=rstd[:], op=ALU.mult)
                 minus_mean_rstd_of[u] = minus_mean_rstd
@@ -179,7 +193,7 @@ def tile_attentionfreetransformerencoder_pb_kernel(
             x_hat = work.tile([P, UNIT, PACK, P], F32)
             for i in range(UNIT):
                 sorted_x = x_sb[u][:, i, :].rearrange("r (p t) -> r t p", t=PACK)
-                if NORM_ENGINES[i] == "scalar":
+                if norm_engine(u, i) == "scalar":
                     nc.scalar.activation(
                         out=x_hat[:, i, :, :],
                         in_=sorted_x,
@@ -188,7 +202,7 @@ def tile_attentionfreetransformerencoder_pb_kernel(
                         bias=minus_mean_rstd_of[u][:, i : i + 1],
                     )
                 else:
-                    engine = nc.vector if NORM_ENGINES[i] == "vector" else nc.gpsimd
+                    engine = nc.vector
                     engine.tensor_scalar(
                         out=x_hat[:, i, :, :],
                         in0=sorted_x,
@@ -199,9 +213,12 @@ def tile_attentionfreetransformerencoder_pb_kernel(
                     )
             x_hat_of[u] = x_hat
 
-        def residual(u):
+        def residual(u, side):
             for i in range(UNIT):
-                nc.gpsimd.tensor_tensor(out=x_bo[u][:, i, :], in0=x_sb[u][:, i, :], in1=bo_all[:], op=ALU.add)
+                if residual_engine(u, i) != side:
+                    continue
+                engine = nc.gpsimd if side == "gpsimd" else nc.vector
+                engine.tensor_tensor(out=x_bo[u][:, i, :], in0=x_sb[u][:, i, :], in1=bo_all[:], op=ALU.add)
 
         def unread_passes(bank, count):
             for n in range(count):
@@ -345,7 +362,6 @@ def tile_attentionfreetransformerencoder_pb_kernel(
                 nc.sync.dma_start(out=out_rows[:, u * UNIT + i, :], in_=o_sb[:])
 
         def constants():
-            nc.vector.tensor_copy(out=gain[:], in_=gain_bf[:])
             nc.vector.tensor_copy(
                 out=wq_perm_words[:].rearrange("p (t m) -> p t m", t=PACK),
                 in_=wq_words[:].bitcast(I32).rearrange("p (m t) -> p t m", t=PACK),
@@ -359,7 +375,7 @@ def tile_attentionfreetransformerencoder_pb_kernel(
         def live(u):
             return 0 <= u < UNITS
 
-        for j in range(-STATS_LEAD, UNITS + 2):
+        for j in range(-4, UNITS + 2):
             if live(j - 1):
                 y_grouped(j - 1)
             if live(j):
@@ -375,14 +391,17 @@ def tile_attentionfreetransformerencoder_pb_kernel(
                 h_by_t(j + 1)
             if live(j):
                 sigmoid_by_t(j)
-            if live(j + STATS_LEAD):
-                stats(j + STATS_LEAD)
-            if j == -2:
-                constants()
             if live(j + NORM_LEAD):
                 normalise(j + NORM_LEAD)
                 x_hat_transposed(j + NORM_LEAD)
             if live(j + 1):
+                residual(j + 1, "vector")
+            if live(j + 4):
+                stats(j + 4)
+                aggregate(j + 4)
+            if j == -1:
+                constants()
+            if live(j + 1):
                 yt_transposed(j + 1)
-            if live(j):
-                residual(j)
+            if live(j + 3):
+                residual(j + 3, "gpsimd")

@@ -38,10 +38,10 @@ def norm_engine(u, i):
 
 
 def residual_engine(u, i):
-    return "vector"
+    return "gpsimd" if u < 4 or i == 0 else "vector"
 
-WARM_Q = 3
-WARM_X = 3
+WARM_Q = 1
+WARM_X = 1
 
 FLOPS = 2 * 2 * ROWS * D * D
 

@@ -17,10 +17,9 @@ D = 512
 PACK = 4
 ROWS = 2048
 TILES = ROWS // P
-UNIT = 2
-UNITS = TILES // UNIT
-UNIT_ROWS = UNIT * P
-PSUM_BANKS = 8
+UNIT_TILES = [2,2,2,2,2,2,2,2]
+UNITS = len(UNIT_TILES)
+FIRST_TILE = [sum(UNIT_TILES[:u]) for u in range(UNITS)]
 QUADRANT = 32
 QUADRANTS = P // QUADRANT
 SCALE_ROWS = 4
@@ -28,9 +27,8 @@ BN_STATS_DIM = 6
 BN_AGGR_DIM = 2
 RUN = 4
 EPS = 1e-5
-STATS_LEAD = 3
-NORM_LEAD = 2
-WARM_FROM = 0
+
+FLOPS = 2 * 2 * ROWS * D * D
 
 
 def norm_engine(u, i):
@@ -39,11 +37,6 @@ def norm_engine(u, i):
 
 def residual_engine(u, i):
     return "gpsimd" if u < 4 or i == 0 else "vector"
-
-WARM_Q = 1
-WARM_X = 1
-
-FLOPS = 2 * 2 * ROWS * D * D
 
 
 def load_weight(nc, words_dram, scales_dram, words, scales):
@@ -83,23 +76,20 @@ def tile_attentionfreetransformerencoder_pb_kernel(
         wq_perm_words = keep.tile([P, D], I32, align_bytes=64)
         wq_perm_scales = keep.tile([P, D], U8, align_bytes=64)
 
-        x_sb = []
-        yt_sb = []
-        x_bo = []
-        for u in range(UNITS):
-            x_unit = keep.tile([P, UNIT, D], BF16, name="x%d" % u)
-            x_sb.append(x_unit)
-            yt_unit = keep.tile([P, UNIT, D], BF16, name="yt%d" % u)
-            yt_sb.append(yt_unit)
-            x_bo_unit = keep.tile([P, UNIT, D], F32, name="x_bo%d" % u)
-            x_bo.append(x_bo_unit)
+        x_all = keep.tile([P, TILES, D], BF16)
+        yt_all = keep.tile([P, TILES, D], BF16)
+        x_bo = keep.tile([P, TILES, D], F32)
+
+        def tiles_of(u):
+            return range(FIRST_TILE[u], FIRST_TILE[u] + UNIT_TILES[u])
 
         def load_rows(dst, src, u):
-            nc.sync.dma_start(out=dst[u][:], in_=src[:, u * UNIT : (u + 1) * UNIT, :])
+            rows = slice(FIRST_TILE[u], FIRST_TILE[u] + UNIT_TILES[u])
+            nc.sync.dma_start(out=dst[:, rows, :], in_=src[:, rows, :])
 
         gain_bf = keep.tile([P, PACK], BF16)
-        shift_bf = keep.tile([P, PACK], BF16)
-        bq_bf = keep.tile([P, PACK], BF16)
+        shift = keep.tile([P, PACK], BF16)
+        bq_col = keep.tile([P, PACK], BF16)
         bo_all = keep.tile([P, D], F32)
 
         bo_row = keep.tile([P, D], BF16)
@@ -107,92 +97,93 @@ def tile_attentionfreetransformerencoder_pb_kernel(
         ones = keep.tile([P, P], BF16)
         nc.gpsimd.memset(ones[:], 1.0)
 
-        load_rows(x_sb, x_rows, 0)
+        load_rows(x_all, x_rows, 0)
         nc.sync.dma_start(out=bo_row[0:1, :], in_=bo.rearrange("(o n) -> o n", o=1))
-        load_rows(x_sb, x_rows, 1)
+        load_rows(x_all, x_rows, 1)
         nc.sync.dma_start(out=gain_bf[:], in_=ln1_g.rearrange("(p t) -> p t", t=PACK))
-        nc.sync.dma_start(out=shift_bf[:], in_=ln1_b.rearrange("(p t) -> p t", t=PACK))
-        load_rows(x_sb, x_rows, 2)
+        nc.sync.dma_start(out=shift[:], in_=ln1_b.rearrange("(p t) -> p t", t=PACK))
+        load_rows(x_all, x_rows, 2)
         load_weight(nc, Wq_words, Wq_scales, wq_words, wq_scales)
-        nc.sync.dma_start(out=bq_bf[:], in_=bq.rearrange("(p t) -> p t", t=PACK))
-        load_rows(yt_sb, yt_rows, 0)
-        load_rows(x_sb, x_rows, 3)
-        load_rows(yt_sb, yt_rows, 1)
+        nc.sync.dma_start(out=bq_col[:], in_=bq.rearrange("(p t) -> p t", t=PACK))
+        load_rows(x_all, x_rows, 3)
+        load_rows(yt_all, yt_rows, 0)
+        load_rows(x_all, x_rows, 4)
+        load_rows(yt_all, yt_rows, 1)
         load_weight(nc, Wo_words, Wo_scales, wo_words, wo_scales)
-        for u in range(4, UNITS):
-            load_rows(x_sb, x_rows, u)
-            load_rows(yt_sb, yt_rows, u - 2)
-        for u in range(UNITS - 2, UNITS):
-            load_rows(yt_sb, yt_rows, u)
+        for u in range(5, UNITS):
+            load_rows(x_all, x_rows, u)
+            load_rows(yt_all, yt_rows, u - 3)
+        for u in range(UNITS - 3, UNITS):
+            load_rows(yt_all, yt_rows, u)
 
         identity = keep.tile([P, P], F32)
         make_identity(nc, identity[:])
-        minus_half = keep.tile([P, UNIT], F32)
+        minus_half = keep.tile([P, 2], F32)
         nc.gpsimd.memset(minus_half[:], -0.5)
 
         warm = keep.tile([P, 1], F32)
         nc.vector.memset(warm[:], 0.0)
         nc.scalar.activation(out=warm[:], in_=warm[:], func=ACT.Sigmoid)
 
-        bo_bank = psum.tile([P, D], F32, tag="o")
-        nc.tensor.matmul(out=bo_bank[:], lhsT=ones[:], rhs=bo_row[:], start=True, stop=True)
-        nc.scalar.copy(out=bo_all[:], in_=bo_bank[:])
-
         gain = keep.tile([P, PACK], F32)
         nc.gpsimd.tensor_copy(out=gain[:], in_=gain_bf[:])
-        shift = shift_bf
-        bq_col = bq_bf
 
         minus_mean_of = {}
-        mean_var_of = {}
+        moments_of = {}
         minus_mean_rstd_of = {}
         rstd_of = {}
         x_hat_of = {}
         x_hat_t_of = {}
         h_by_t_of = {}
         h_grouped_of = {}
-        h_words_of = {}
-        h_scales_of = {}
+        h_quantised_of = {}
         q_t_of = {}
         sig_by_t_of = {}
         yt_t_of = {}
         y_grouped_of = {}
-        y_words_of = {}
-        y_scales_of = {}
+        y_quantised_of = {}
         o_bank_of = {}
 
+        def spread_bo():
+            bo_bank = psum.tile([P, D], F32, tag="o")
+            nc.tensor.matmul(out=bo_bank[:], lhsT=ones[:], rhs=bo_row[:], start=True, stop=True)
+            nc.scalar.copy(out=bo_all[:], in_=bo_bank[:])
+
         def stats(u):
-            moments = small.tile([P, UNIT, BN_STATS_DIM], F32)
-            mean_var = small.tile([P, UNIT, BN_AGGR_DIM], F32)
-            for i in range(UNIT):
-                nc.vector.bn_stats(out=moments[:, i, :], in_=x_sb[u][:, i, :])
-            mean_var_of[u] = (moments, mean_var)
+            n = UNIT_TILES[u]
+            moments = small.tile([P, 2, BN_STATS_DIM], F32)
+            for i, row in enumerate(tiles_of(u)):
+                nc.vector.bn_stats(out=moments[:, i, :], in_=x_all[:, row, :])
+            moments_of[u] = moments
 
         def aggregate(u):
-            moments, mean_var = mean_var_of[u]
-            for i in range(UNIT):
-                nc.vector.bn_aggr(out=mean_var[:, i, :], in_=moments[:, i, :])
-            var_eps = small.tile([P, UNIT], F32)
-            rstd = small.tile([P, UNIT], F32)
+            n = UNIT_TILES[u]
+            mean_var = small.tile([P, 2, BN_AGGR_DIM], F32)
+            for i in range(n):
+                nc.vector.bn_aggr(out=mean_var[:, i, :], in_=moments_of[u][:, i, :])
+            var_eps = small.tile([P, 2], F32)
+            rstd = small.tile([P, 2], F32)
             nc.gpsimd.tensor_scalar(
-                out=var_eps[:], in0=mean_var[:, :, 1], scalar1=1.0, scalar2=EPS, op0=ALU.mult, op1=ALU.add
+                out=var_eps[:, 0:n], in0=mean_var[:, 0:n, 1], scalar1=1.0, scalar2=EPS, op0=ALU.mult, op1=ALU.add
             )
-            nc.gpsimd.tensor_tensor(out=rstd[:], in0=var_eps[:], in1=minus_half[:], op=ALU.pow)
-            minus_mean = small.tile([P, UNIT], F32)
+            nc.gpsimd.tensor_tensor(out=rstd[:, 0:n], in0=var_eps[:, 0:n], in1=minus_half[:, 0:n], op=ALU.pow)
+            minus_mean = small.tile([P, 2], F32)
             nc.gpsimd.tensor_scalar(
-                out=minus_mean[:], in0=mean_var[:, :, 0], scalar1=-1.0, scalar2=0.0, op0=ALU.mult, op1=ALU.add
+                out=minus_mean[:, 0:n], in0=mean_var[:, 0:n, 0], scalar1=-1.0, scalar2=0.0, op0=ALU.mult, op1=ALU.add
             )
+            minus_mean_rstd = small.tile([P, 2], F32)
+            if "scalar" in [norm_engine(u, i) for i in range(n)]:
+                nc.gpsimd.tensor_tensor(
+                    out=minus_mean_rstd[:, 0:n], in0=minus_mean[:, 0:n], in1=rstd[:, 0:n], op=ALU.mult
+                )
             minus_mean_of[u] = minus_mean
-            if "scalar" in [norm_engine(u, i) for i in range(UNIT)]:
-                minus_mean_rstd = small.tile([P, UNIT], F32)
-                nc.gpsimd.tensor_tensor(out=minus_mean_rstd[:], in0=minus_mean[:], in1=rstd[:], op=ALU.mult)
-                minus_mean_rstd_of[u] = minus_mean_rstd
+            minus_mean_rstd_of[u] = minus_mean_rstd
             rstd_of[u] = rstd
 
         def normalise(u):
-            x_hat = work.tile([P, UNIT, PACK, P], F32)
-            for i in range(UNIT):
-                sorted_x = x_sb[u][:, i, :].rearrange("r (p t) -> r t p", t=PACK)
+            x_hat = work.tile([P, 2, PACK, P], F32)
+            for i, row in enumerate(tiles_of(u)):
+                sorted_x = x_all[:, row, :].rearrange("r (p t) -> r t p", t=PACK)
                 if norm_engine(u, i) == "scalar":
                     nc.scalar.activation(
                         out=x_hat[:, i, :, :],
@@ -202,8 +193,7 @@ def tile_attentionfreetransformerencoder_pb_kernel(
                         bias=minus_mean_rstd_of[u][:, i : i + 1],
                     )
                 else:
-                    engine = nc.vector
-                    engine.tensor_scalar(
+                    nc.vector.tensor_scalar(
                         out=x_hat[:, i, :, :],
                         in0=sorted_x,
                         scalar1=minus_mean_of[u][:, i : i + 1],
@@ -214,11 +204,11 @@ def tile_attentionfreetransformerencoder_pb_kernel(
             x_hat_of[u] = x_hat
 
         def residual(u, side):
-            for i in range(UNIT):
+            for i, row in enumerate(tiles_of(u)):
                 if residual_engine(u, i) != side:
                     continue
                 engine = nc.gpsimd if side == "gpsimd" else nc.vector
-                engine.tensor_tensor(out=x_bo[u][:, i, :], in0=x_sb[u][:, i, :], in1=bo_all[:], op=ALU.add)
+                engine.tensor_tensor(out=x_bo[:, row, :], in0=x_all[:, row, :], in1=bo_all[:], op=ALU.add)
 
         def unread_passes(bank, count):
             for n in range(count):
@@ -235,11 +225,11 @@ def tile_attentionfreetransformerencoder_pb_kernel(
         def x_hat_transposed(u):
             banks = []
             for pair in range(PACK // 2):
-                bank = psum.tile([P, 2, UNIT_ROWS], F32, tag="x")
-                if pair == 0 and u >= WARM_FROM + NORM_LEAD:
-                    unread_passes(bank, WARM_X)
+                bank = psum.tile([P, 2, 2 * P], F32, tag="x")
+                if pair == 0 and u >= 2:
+                    unread_passes(bank, 1)
                 for e in range(2):
-                    for i in range(UNIT):
+                    for i in range(UNIT_TILES[u]):
                         nc.tensor.transpose(
                             bank[:, e, i * P : (i + 1) * P], x_hat_of[u][:, i, 2 * pair + e, :], identity[:]
                         )
@@ -247,11 +237,12 @@ def tile_attentionfreetransformerencoder_pb_kernel(
             x_hat_t_of[u] = banks
 
         def h_by_t(u):
-            by_t = work.tile([P, PACK, UNIT_ROWS], BF16)
+            rows = UNIT_TILES[u] * P
+            by_t = work.tile([P, PACK, rows], BF16, name="h_by_t_%d" % rows)
             for t in range(PACK):
                 nc.scalar.activation(
                     out=by_t[:, t, :],
-                    in_=x_hat_t_of[u][t // 2][:, t % 2, :],
+                    in_=x_hat_t_of[u][t // 2][:, t % 2, 0:rows],
                     func=ACT.Identity,
                     scale=gain[:, t : t + 1],
                     bias=shift[:, t : t + 1],
@@ -259,41 +250,43 @@ def tile_attentionfreetransformerencoder_pb_kernel(
             h_by_t_of[u] = by_t
 
         def h_grouped(u):
-            grouped = work.tile([P, UNIT_ROWS, PACK], BF16, align_bytes=64)
+            rows = UNIT_TILES[u] * P
+            grouped = work.tile([P, rows, PACK], BF16, align_bytes=64, name="h_grouped_%d" % rows)
             nc.scalar.copy(
                 out=grouped[:].rearrange("p (c i) t -> p c t i", i=RUN),
                 in_=h_by_t_of[u][:].rearrange("p t (c i) -> p c t i", i=RUN),
             )
             h_grouped_of[u] = grouped
 
-        def quantise(grouped, words, scales):
+        def quantise(grouped, rows, name):
+            words = work.tile([P, rows], U32, align_bytes=64, name="%s_words_%d" % (name, rows))
+            scales = work.tile([P, rows], U8, align_bytes=64, name="%s_scales_%d" % (name, rows))
             nc.vector.quantize_mx(
                 out=words[:].bitcast(FP8X4),
                 scales=scales[:],
                 in_=grouped[:].rearrange("p r t -> p (r t)"),
             )
+            return words, scales
 
         def h_quantised(u):
-            h_words = work.tile([P, UNIT_ROWS], U32, align_bytes=64)
-            h_scales = work.tile([P, UNIT_ROWS], U8, align_bytes=64)
-            quantise(h_grouped_of[u], h_words, h_scales)
-            h_words_of[u] = h_words
-            h_scales_of[u] = h_scales
+            h_quantised_of[u] = quantise(h_grouped_of[u], UNIT_TILES[u] * P, "h")
 
         def q_transposed(u):
+            rows = UNIT_TILES[u] * P
+            words, scales = h_quantised_of[u]
             banks = []
             for pair in range(PACK // 2):
-                bank = psum.tile([P, 2, UNIT_ROWS], F32, tag="q")
-                if pair == 0 and u >= WARM_FROM:
-                    unread_passes(bank, WARM_Q)
+                bank = psum.tile([P, 2, 2 * P], F32, tag="q")
+                if pair == 0:
+                    unread_passes(bank, 1)
                 for e in range(2):
                     t = 2 * pair + e
                     nc.tensor.matmul_mx(
-                        out=bank[:, e, :],
+                        out=bank[:, e, 0:rows],
                         lhsT=wq_perm_words[:, t * P : (t + 1) * P].bitcast(FP8X4),
                         lhsT_scale=wq_perm_scales[:, t * P : (t + 1) * P],
-                        rhs=h_words_of[u][:].bitcast(FP8X4),
-                        rhs_scale=h_scales_of[u][:],
+                        rhs=words[:].bitcast(FP8X4),
+                        rhs_scale=scales[:],
                         start=True,
                         stop=True,
                     )
@@ -301,52 +294,53 @@ def tile_attentionfreetransformerencoder_pb_kernel(
             q_t_of[u] = banks
 
         def sigmoid_by_t(u):
-            sig_by_t = work.tile([P, PACK, UNIT_ROWS], F32)
+            rows = UNIT_TILES[u] * P
+            sig_by_t = work.tile([P, PACK, rows], F32, name="sig_by_t_%d" % rows)
             for t in range(PACK):
                 nc.scalar.activation(
                     out=sig_by_t[:, t, :],
-                    in_=q_t_of[u][t // 2][:, t % 2, :],
+                    in_=q_t_of[u][t // 2][:, t % 2, 0:rows],
                     func=ACT.Sigmoid,
                     bias=bq_col[:, t : t + 1],
                 )
             sig_by_t_of[u] = sig_by_t
 
         def yt_transposed(u):
-            yt_t = psum.tile([P, 2, UNIT, P], F32, tag="yt")
+            n = UNIT_TILES[u]
+            yt_t = psum.tile([P, 4 * P], F32, tag="yt")
             for w in range(2):
-                for i in range(UNIT):
-                    yt_words = yt_sb[u][:, i, :].bitcast(F32).rearrange("r (p w) -> r w p", w=2)
-                    nc.tensor.transpose(yt_t[:, w, i, :], yt_words[:, w, :], identity[:])
+                for i, row in enumerate(tiles_of(u)):
+                    yt_words = yt_all[:, row, :].bitcast(F32).rearrange("r (p w) -> r w p", w=2)
+                    nc.tensor.transpose(
+                        yt_t[:, 2 * i * P : 2 * (i + 1) * P].rearrange("p (r w) -> p w r", w=2)[:, w, :],
+                        yt_words[:, w, :],
+                        identity[:],
+                    )
             yt_t_of[u] = yt_t
 
         def y_grouped(u):
-            grouped = work.tile([P, UNIT_ROWS, PACK], BF16, align_bytes=64, name="y_grouped")
+            rows = UNIT_TILES[u] * P
+            grouped = work.tile([P, rows, PACK], BF16, align_bytes=64, name="y_grouped_%d" % rows)
             nc.vector.tensor_tensor(
-                out=grouped[:].rearrange("p r (w e) -> p r w e", e=2),
-                in0=sig_by_t_of[u][:].rearrange("p (w e) r -> p r w e", e=2),
-                in1=yt_t_of[u][:]
-                .rearrange("p w i r -> p (w i r)")
-                .bitcast(BF16)
-                .rearrange("p (w r e) -> p r w e", w=2, e=2),
+                out=grouped[:].rearrange("p (c i) t -> p c t i", i=RUN),
+                in0=sig_by_t_of[u][:].rearrange("p t (c i) -> p c t i", i=RUN),
+                in1=yt_t_of[u][:, 0 : 2 * rows].bitcast(BF16).rearrange("p (c i t) -> p c t i", i=RUN, t=PACK),
                 op=ALU.mult,
             )
             y_grouped_of[u] = grouped
 
         def y_quantised(u):
-            y_words = work.tile([P, UNIT_ROWS], U32, align_bytes=64)
-            y_scales = work.tile([P, UNIT_ROWS], U8, align_bytes=64)
-            quantise(y_grouped_of[u], y_words, y_scales)
-            y_words_of[u] = y_words
-            y_scales_of[u] = y_scales
+            y_quantised_of[u] = quantise(y_grouped_of[u], UNIT_TILES[u] * P, "y")
 
         def projected(u):
+            words, scales = y_quantised_of[u]
             banks = []
-            for i in range(UNIT):
+            for i in range(UNIT_TILES[u]):
                 o_bank = psum.tile([P, D], F32, tag="o")
                 nc.tensor.matmul_mx(
                     out=o_bank[:],
-                    lhsT=y_words_of[u][:, i * P : (i + 1) * P].bitcast(FP8X4),
-                    lhsT_scale=y_scales_of[u][:, i * P : (i + 1) * P],
+                    lhsT=words[:, i * P : (i + 1) * P].bitcast(FP8X4),
+                    lhsT_scale=scales[:, i * P : (i + 1) * P],
                     rhs=wo_words[:].bitcast(FP8X4),
                     rhs_scale=wo_scales[:],
                     start=True,
@@ -356,10 +350,10 @@ def tile_attentionfreetransformerencoder_pb_kernel(
             o_bank_of[u] = banks
 
         def stored(u):
-            for i in range(UNIT):
+            for i, row in enumerate(tiles_of(u)):
                 o_sb = work.tile([P, D], F32)
-                nc.vector.tensor_tensor(out=o_sb[:], in0=o_bank_of[u][i][:], in1=x_bo[u][:, i, :], op=ALU.add)
-                nc.sync.dma_start(out=out_rows[:, u * UNIT + i, :], in_=o_sb[:])
+                nc.vector.tensor_tensor(out=o_sb[:], in0=o_bank_of[u][i][:], in1=x_bo[:, row, :], op=ALU.add)
+                nc.sync.dma_start(out=out_rows[:, row, :], in_=o_sb[:])
 
         def constants():
             nc.vector.tensor_copy(
@@ -376,28 +370,35 @@ def tile_attentionfreetransformerencoder_pb_kernel(
             return 0 <= u < UNITS
 
         for j in range(-4, UNITS + 2):
+            if j == -3:
+                spread_bo()
             if live(j - 1):
                 y_grouped(j - 1)
             if live(j):
                 h_grouped(j)
+            if live(j):
                 h_quantised(j)
+            if live(j):
                 q_transposed(j)
             if live(j - 2):
                 stored(j - 2)
             if live(j - 1):
                 y_quantised(j - 1)
+            if live(j - 1):
                 projected(j - 1)
             if live(j + 1):
                 h_by_t(j + 1)
+            if live(j + 4):
+                stats(j + 4)
+            if live(j + 2):
+                normalise(j + 2)
+            if live(j + 2):
+                x_hat_transposed(j + 2)
             if live(j):
                 sigmoid_by_t(j)
-            if live(j + NORM_LEAD):
-                normalise(j + NORM_LEAD)
-                x_hat_transposed(j + NORM_LEAD)
             if live(j + 1):
                 residual(j + 1, "vector")
             if live(j + 4):
-                stats(j + 4)
                 aggregate(j + 4)
             if j == -1:
                 constants()

@@ -36,7 +36,7 @@ def norm_engine(u, i):
 
 
 def residual_engine(u, i):
-    return "gpsimd" if u < 4 or i == 0 else "vector"
+    return "gpsimd"
 
 
 def load_weight(nc, words_dram, scales_dram, words, scales):
@@ -227,7 +227,7 @@ def tile_attentionfreetransformerencoder_pb_kernel(
             for pair in range(PACK // 2):
                 bank = psum.tile([P, 2, 2 * P], F32, tag="x")
                 if pair == 0 and u >= 2:
-                    unread_passes(bank, 1)
+                    unread_passes(bank, 3)
                 for e in range(2):
                     for i in range(UNIT_TILES[u]):
                         nc.tensor.transpose(
@@ -278,7 +278,7 @@ def tile_attentionfreetransformerencoder_pb_kernel(
             for pair in range(PACK // 2):
                 bank = psum.tile([P, 2, 2 * P], F32, tag="q")
                 if pair == 0:
-                    unread_passes(bank, 1)
+                    unread_passes(bank, 3)
                 for e in range(2):
                     t = 2 * pair + e
                     nc.tensor.matmul_mx(
@@ -372,28 +372,28 @@ def tile_attentionfreetransformerencoder_pb_kernel(
         for j in range(-4, UNITS + 2):
             if j == -3:
                 spread_bo()
-            if live(j - 1):
-                y_grouped(j - 1)
-            if live(j):
-                h_grouped(j)
+            if live(j + 1):
+                h_by_t(j + 1)
+            if live(j + 1):
+                h_grouped(j + 1)
             if live(j):
                 h_quantised(j)
             if live(j):
                 q_transposed(j)
+            if live(j + 2):
+                normalise(j + 2)
+            if live(j + 2):
+                x_hat_transposed(j + 2)
+            if live(j + 4):
+                stats(j + 4)
+            if live(j - 1):
+                y_grouped(j - 1)
             if live(j - 2):
                 stored(j - 2)
             if live(j - 1):
                 y_quantised(j - 1)
             if live(j - 1):
                 projected(j - 1)
-            if live(j + 1):
-                h_by_t(j + 1)
-            if live(j + 4):
-                stats(j + 4)
-            if live(j + 2):
-                normalise(j + 2)
-            if live(j + 2):
-                x_hat_transposed(j + 2)
             if live(j):
                 sigmoid_by_t(j)
             if live(j + 1):

@@ -36,7 +36,7 @@ def norm_engine(u, i):
 
 
 def residual_engine(u, i):
-    return "gpsimd"
+    return "vector" if i else "gpsimd"
 
 
 def load_weight(nc, words_dram, scales_dram, words, scales):
@@ -404,5 +404,5 @@ def tile_attentionfreetransformerencoder_pb_kernel(
                 constants()
             if live(j + 1):
                 yt_transposed(j + 1)
-            if live(j + 3):
-                residual(j + 3, "gpsimd")
+            if live(j + 1):
+                residual(j + 1, "gpsimd")

@@ -32,11 +32,11 @@ FLOPS = 2 * 2 * ROWS * D * D
 
 
 def norm_engine(u, i):
-    return "scalar" if i else "vector"
+    return "scalar" if i and u < 4 else "vector"
 
 
 def residual_engine(u, i):
-    return "vector" if i else "gpsimd"
+    return "vector" if i and u % 2 else "gpsimd"
 
 
 def load_weight(nc, words_dram, scales_dram, words, scales):
@@ -126,7 +126,6 @@ def tile_attentionfreetransformerencoder_pb_kernel(
         nc.scalar.activation(out=warm[:], in_=warm[:], func=ACT.Sigmoid)
 
         gain = keep.tile([P, PACK], F32)
-        nc.gpsimd.tensor_copy(out=gain[:], in_=gain_bf[:])
 
         minus_mean_of = {}
         moments_of = {}
@@ -293,17 +292,20 @@ def tile_attentionfreetransformerencoder_pb_kernel(
                 banks.append(bank)
             q_t_of[u] = banks
 
-        def sigmoid_by_t(u):
-            rows = UNIT_TILES[u] * P
+        def parts(u):
+            return [(0, 1), (1, 1)] if u == UNITS - 1 else [(0, UNIT_TILES[u])]
+
+        def sigmoid_by_t(u, first, n):
+            rows = n * P
             sig_by_t = work.tile([P, PACK, rows], F32, name="sig_by_t_%d" % rows)
             for t in range(PACK):
                 nc.scalar.activation(
                     out=sig_by_t[:, t, :],
-                    in_=q_t_of[u][t // 2][:, t % 2, 0:rows],
+                    in_=q_t_of[u][t // 2][:, t % 2, first * P : first * P + rows],
                     func=ACT.Sigmoid,
                     bias=bq_col[:, t : t + 1],
                 )
-            sig_by_t_of[u] = sig_by_t
+            sig_by_t_of[u, first] = sig_by_t
 
         def yt_transposed(u):
             n = UNIT_TILES[u]
@@ -318,24 +320,24 @@ def tile_attentionfreetransformerencoder_pb_kernel(
                     )
             yt_t_of[u] = yt_t
 
-        def y_grouped(u):
-            rows = UNIT_TILES[u] * P
+        def y_grouped(u, first, n):
+            rows = n * P
             grouped = work.tile([P, rows, PACK], BF16, align_bytes=64, name="y_grouped_%d" % rows)
             nc.vector.tensor_tensor(
                 out=grouped[:].rearrange("p (c i) t -> p c t i", i=RUN),
-                in0=sig_by_t_of[u][:].rearrange("p t (c i) -> p c t i", i=RUN),
-                in1=yt_t_of[u][:, 0 : 2 * rows].bitcast(BF16).rearrange("p (c i t) -> p c t i", i=RUN, t=PACK),
+                in0=sig_by_t_of[u, first][:].rearrange("p t (c i) -> p c t i", i=RUN),
+                in1=yt_t_of[u][:, 2 * first * P : 2 * first * P + 2 * rows].bitcast(BF16).rearrange("p (c i t) -> p c t i", i=RUN, t=PACK),
                 op=ALU.mult,
             )
-            y_grouped_of[u] = grouped
+            y_grouped_of[u, first] = grouped
 
-        def y_quantised(u):
-            y_quantised_of[u] = quantise(y_grouped_of[u], UNIT_TILES[u] * P, "y")
+        def y_quantised(u, first, n):
+            y_quantised_of[u, first] = quantise(y_grouped_of[u, first], n * P, "y")
 
-        def projected(u):
-            words, scales = y_quantised_of[u]
+        def projected(u, first, n):
+            words, scales = y_quantised_of[u, first]
             banks = []
-            for i in range(UNIT_TILES[u]):
+            for i in range(n):
                 o_bank = psum.tile([P, D], F32, tag="o")
                 nc.tensor.matmul_mx(
                     out=o_bank[:],
@@ -347,7 +349,7 @@ def tile_attentionfreetransformerencoder_pb_kernel(
                     stop=True,
                 )
                 banks.append(o_bank)
-            o_bank_of[u] = banks
+            o_bank_of[u] = o_bank_of.get(u, []) + banks
 
         def stored(u):
             for i, row in enumerate(tiles_of(u)):
@@ -355,16 +357,18 @@ def tile_attentionfreetransformerencoder_pb_kernel(
                 nc.vector.tensor_tensor(out=o_sb[:], in0=o_bank_of[u][i][:], in1=x_bo[:, row, :], op=ALU.add)
                 nc.sync.dma_start(out=out_rows[:, row, :], in_=o_sb[:])
 
+        def cast_gain():
+            nc.vector.tensor_copy(out=gain[:], in_=gain_bf[:])
+
         def constants():
             nc.vector.tensor_copy(
                 out=wq_perm_words[:].rearrange("p (t m) -> p t m", t=PACK),
                 in_=wq_words[:].bitcast(I32).rearrange("p (m t) -> p t m", t=PACK),
             )
-            for t in range(PACK):
-                nc.vector.tensor_copy(
-                    out=wq_perm_scales[:, t * P : (t + 1) * P],
-                    in_=wq_scales[:].rearrange("p (m t) -> p t m", t=PACK)[:, t, :],
-                )
+            nc.vector.tensor_copy(
+                out=wq_perm_scales[:].rearrange("p (t m) -> p t m", t=PACK),
+                in_=wq_scales[:].rearrange("p (m t) -> p t m", t=PACK),
+            )
 
         def live(u):
             return 0 <= u < UNITS
@@ -387,19 +391,25 @@ def tile_attentionfreetransformerencoder_pb_kernel(
             if live(j + 4):
                 stats(j + 4)
             if live(j - 1):
-                y_grouped(j - 1)
+                for part in parts(j - 1):
+                    y_grouped(j - 1, *part)
             if live(j - 2):
                 stored(j - 2)
-            if live(j - 1):
-                y_quantised(j - 1)
-            if live(j - 1):
-                projected(j - 1)
-            if live(j):
-                sigmoid_by_t(j)
-            if live(j + 1):
-                residual(j + 1, "vector")
             if live(j + 4):
                 aggregate(j + 4)
+            if live(j - 1):
+                for part in parts(j - 1):
+                    y_quantised(j - 1, *part)
+            if live(j - 1):
+                for part in parts(j - 1):
+                    projected(j - 1, *part)
+            if live(j):
+                for part in parts(j):
+                    sigmoid_by_t(j, *part)
+            if live(j + 1):
+                residual(j + 1, "vector")
+            if j == -3:
+                cast_gain()
             if j == -1:
                 constants()
             if live(j + 1):

@@ -32,7 +32,7 @@ FLOPS = 2 * 2 * ROWS * D * D
 
 
 def norm_engine(u, i):
-    return "scalar" if i and u < 4 else "vector"
+    return "scalar" if i and u < 2 else "vector"
 
 
 def residual_engine(u, i):
@@ -226,7 +226,7 @@ def tile_attentionfreetransformerencoder_pb_kernel(
             for pair in range(PACK // 2):
                 bank = psum.tile([P, 2, 2 * P], F32, tag="x")
                 if pair == 0 and u >= 2:
-                    unread_passes(bank, 3)
+                    unread_passes(bank, 2)
                 for e in range(2):
                     for i in range(UNIT_TILES[u]):
                         nc.tensor.transpose(
@@ -276,8 +276,6 @@ def tile_attentionfreetransformerencoder_pb_kernel(
             banks = []
             for pair in range(PACK // 2):
                 bank = psum.tile([P, 2, 2 * P], F32, tag="q")
-                if pair == 0:
-                    unread_passes(bank, 3)
                 for e in range(2):
                     t = 2 * pair + e
                     nc.tensor.matmul_mx(
@@ -373,8 +371,8 @@ def tile_attentionfreetransformerencoder_pb_kernel(
         def live(u):
             return 0 <= u < UNITS
 
-        for j in range(-4, UNITS + 2):
-            if j == -3:
+        for j in range(-5, UNITS + 2):
+            if j == -4:
                 spread_bo()
             if live(j + 1):
                 h_by_t(j + 1)
@@ -384,19 +382,19 @@ def tile_attentionfreetransformerencoder_pb_kernel(
                 h_quantised(j)
             if live(j):
                 q_transposed(j)
-            if live(j + 2):
-                normalise(j + 2)
+            if live(j + 3):
+                normalise(j + 3)
             if live(j + 2):
                 x_hat_transposed(j + 2)
-            if live(j + 4):
-                stats(j + 4)
+            if live(j + 5):
+                stats(j + 5)
             if live(j - 1):
                 for part in parts(j - 1):
                     y_grouped(j - 1, *part)
             if live(j - 2):
                 stored(j - 2)
-            if live(j + 4):
-                aggregate(j + 4)
+            if live(j + 5):
+                aggregate(j + 5)
             if live(j - 1):
                 for part in parts(j - 1):
                     y_quantised(j - 1, *part)
@@ -408,9 +406,9 @@ def tile_attentionfreetransformerencoder_pb_kernel(
                     sigmoid_by_t(j, *part)
             if live(j + 1):
                 residual(j + 1, "vector")
-            if j == -3:
+            if j == -4:
                 cast_gain()
-            if j == -1:
+            if j == -2:
                 constants()
             if live(j + 1):
                 yt_transposed(j + 1)

@@ -97,23 +97,25 @@ def tile_attentionfreetransformerencoder_pb_kernel(
         ones = keep.tile([P, P], BF16)
         nc.gpsimd.memset(ones[:], 1.0)
 
-        load_rows(x_all, x_rows, 0)
-        nc.sync.dma_start(out=bo_row[0:1, :], in_=bo.rearrange("(o n) -> o n", o=1))
+        for row in tiles_of(0):
+            nc.sync.dma_start(out=x_all[:, row, :], in_=x_rows[:, row, :])
         load_rows(x_all, x_rows, 1)
         nc.sync.dma_start(out=gain_bf[:], in_=ln1_g.rearrange("(p t) -> p t", t=PACK))
         nc.sync.dma_start(out=shift[:], in_=ln1_b.rearrange("(p t) -> p t", t=PACK))
         load_rows(x_all, x_rows, 2)
+        load_rows(x_all, x_rows, 3)
+        nc.sync.dma_start(out=bo_row[0:1, :], in_=bo.rearrange("(o n) -> o n", o=1))
         load_weight(nc, Wq_words, Wq_scales, wq_words, wq_scales)
         nc.sync.dma_start(out=bq_col[:], in_=bq.rearrange("(p t) -> p t", t=PACK))
-        load_rows(x_all, x_rows, 3)
-        load_rows(yt_all, yt_rows, 0)
         load_rows(x_all, x_rows, 4)
+        load_rows(yt_all, yt_rows, 0)
+        load_rows(x_all, x_rows, 5)
         load_rows(yt_all, yt_rows, 1)
         load_weight(nc, Wo_words, Wo_scales, wo_words, wo_scales)
-        for u in range(5, UNITS):
+        for u in range(6, UNITS):
             load_rows(x_all, x_rows, u)
-            load_rows(yt_all, yt_rows, u - 3)
-        for u in range(UNITS - 3, UNITS):
+            load_rows(yt_all, yt_rows, u - 4)
+        for u in range(UNITS - 4, UNITS):
             load_rows(yt_all, yt_rows, u)
 
         identity = keep.tile([P, P], F32)
@@ -226,7 +228,7 @@ def tile_attentionfreetransformerencoder_pb_kernel(
             for pair in range(PACK // 2):
                 bank = psum.tile([P, 2, 2 * P], F32, tag="x")
                 if pair == 0 and u >= 2:
-                    unread_passes(bank, 2)
+                    unread_passes(bank, 3)
                 for e in range(2):
                     for i in range(UNIT_TILES[u]):
                         nc.tensor.transpose(
@@ -276,6 +278,8 @@ def tile_attentionfreetransformerencoder_pb_kernel(
             banks = []
             for pair in range(PACK // 2):
                 bank = psum.tile([P, 2, 2 * P], F32, tag="q")
+                if pair == 0:
+                    unread_passes(bank, 3)
                 for e in range(2):
                     t = 2 * pair + e
                     nc.tensor.matmul_mx(
@@ -352,8 +356,13 @@ def tile_attentionfreetransformerencoder_pb_kernel(
         def stored(u):
             for i, row in enumerate(tiles_of(u)):
                 o_sb = work.tile([P, D], F32)
-                nc.vector.tensor_tensor(out=o_sb[:], in0=o_bank_of[u][i][:], in1=x_bo[:, row, :], op=ALU.add)
-                nc.sync.dma_start(out=out_rows[:, row, :], in_=o_sb[:])
+                pieces = 2 if row == TILES - 1 else 1
+                for piece in range(pieces):
+                    columns = slice(piece * D // pieces, (piece + 1) * D // pieces)
+                    nc.vector.tensor_tensor(
+                        out=o_sb[:, columns], in0=o_bank_of[u][i][:, columns], in1=x_bo[:, row, columns], op=ALU.add
+                    )
+                    nc.sync.dma_start(out=out_rows[:, row, columns], in_=o_sb[:, columns])
 
         def cast_gain():
             nc.vector.tensor_copy(out=gain[:], in_=gain_bf[:])
@@ -372,8 +381,6 @@ def tile_attentionfreetransformerencoder_pb_kernel(
             return 0 <= u < UNITS
 
         for j in range(-5, UNITS + 2):
-            if j == -4:
-                spread_bo()
             if live(j + 1):
                 h_by_t(j + 1)
             if live(j + 1):
@@ -391,7 +398,7 @@ def tile_attentionfreetransformerencoder_pb_kernel(
             if live(j - 1):
                 for part in parts(j - 1):
                     y_grouped(j - 1, *part)
-            if live(j - 2):
+            if live(j - 2) and j != UNITS:
                 stored(j - 2)
             if live(j + 5):
                 aggregate(j + 5)
@@ -401,6 +408,8 @@ def tile_attentionfreetransformerencoder_pb_kernel(
             if live(j - 1):
                 for part in parts(j - 1):
                     projected(j - 1, *part)
+            if j == UNITS:
+                stored(j - 2)
             if live(j):
                 for part in parts(j):
                     sigmoid_by_t(j, *part)
@@ -409,6 +418,8 @@ def tile_attentionfreetransformerencoder_pb_kernel(
             if j == -4:
                 cast_gain()
             if j == -2:
+                spread_bo()
+            if j == -1:
                 constants()
             if live(j + 1):
                 yt_transposed(j + 1)

@@ -32,11 +32,11 @@ FLOPS = 2 * 2 * ROWS * D * D
 
 
 def norm_engine(u, i):
-    return "scalar" if i and u < 2 else "vector"
+    return "vector"
 
 
 def residual_engine(u, i):
-    return "vector" if i and u % 2 else "gpsimd"
+    return "gpsimd"
 
 
 def load_weight(nc, words_dram, scales_dram, words, scales):
@@ -120,7 +120,7 @@ def tile_attentionfreetransformerencoder_pb_kernel(
 
         identity = keep.tile([P, P], F32)
         make_identity(nc, identity[:])
-        minus_half = keep.tile([P, 2], F32)
+        minus_half = keep.tile([P, 4], F32)
         nc.gpsimd.memset(minus_half[:], -0.5)
 
         warm = keep.tile([P, 1], F32)
@@ -129,7 +129,8 @@ def tile_attentionfreetransformerencoder_pb_kernel(
 
         gain = keep.tile([P, PACK], F32)
 
-        minus_mean_of = {}
+        mean_var_of = {}
+        mean_of = {}
         moments_of = {}
         minus_mean_rstd_of = {}
         rstd_of = {}
@@ -157,29 +158,36 @@ def tile_attentionfreetransformerencoder_pb_kernel(
                 nc.vector.bn_stats(out=moments[:, i, :], in_=x_all[:, row, :])
             moments_of[u] = moments
 
+        def group_of(u):
+            first = u - (u - 1) % 2 if u >= 1 else u
+            last = min(first + 1, UNITS - 1) if u >= 1 else u
+            return first, last
+
         def aggregate(u):
-            n = UNIT_TILES[u]
-            mean_var = small.tile([P, 2, BN_AGGR_DIM], F32)
-            for i in range(n):
-                nc.vector.bn_aggr(out=mean_var[:, i, :], in_=moments_of[u][:, i, :])
-            var_eps = small.tile([P, 2], F32)
-            rstd = small.tile([P, 2], F32)
+            first, last = group_of(u)
+            if u == first:
+                mean_var = small.tile([P, 4, BN_AGGR_DIM], F32)
+                mean_var_of[first] = mean_var
+            for i in range(2):
+                nc.vector.bn_aggr(out=mean_var_of[first][:, 2 * (u - first) + i, :], in_=moments_of[u][:, i, :])
+            if u < last:
+                return
+            n = 2 * (last - first + 1)
+            mean_var = mean_var_of[first]
+            var_eps = small.tile([P, 4], F32)
+            rstd = small.tile([P, 4], F32)
             nc.gpsimd.tensor_scalar(
                 out=var_eps[:, 0:n], in0=mean_var[:, 0:n, 1], scalar1=1.0, scalar2=EPS, op0=ALU.mult, op1=ALU.add
             )
             nc.gpsimd.tensor_tensor(out=rstd[:, 0:n], in0=var_eps[:, 0:n], in1=minus_half[:, 0:n], op=ALU.pow)
-            minus_mean = small.tile([P, 2], F32)
+            minus_mean = small.tile([P, 4], F32)
             nc.gpsimd.tensor_scalar(
                 out=minus_mean[:, 0:n], in0=mean_var[:, 0:n, 0], scalar1=-1.0, scalar2=0.0, op0=ALU.mult, op1=ALU.add
             )
-            minus_mean_rstd = small.tile([P, 2], F32)
-            if "scalar" in [norm_engine(u, i) for i in range(n)]:
-                nc.gpsimd.tensor_tensor(
-                    out=minus_mean_rstd[:, 0:n], in0=minus_mean[:, 0:n], in1=rstd[:, 0:n], op=ALU.mult
-                )
-            minus_mean_of[u] = minus_mean
-            minus_mean_rstd_of[u] = minus_mean_rstd
-            rstd_of[u] = rstd
+            for v in range(first, last + 1):
+                k = 2 * (v - first)
+                rstd_of[v] = rstd[:, k : k + 2]
+                mean_of[v] = minus_mean[:, k : k + 2]
 
         def normalise(u):
             x_hat = work.tile([P, 2, PACK, P], F32)
@@ -197,7 +205,7 @@ def tile_attentionfreetransformerencoder_pb_kernel(
                     nc.vector.tensor_scalar(
                         out=x_hat[:, i, :, :],
                         in0=sorted_x,
-                        scalar1=minus_mean_of[u][:, i : i + 1],
+                        scalar1=mean_of[u][:, i : i + 1],
                         scalar2=rstd_of[u][:, i : i + 1],
                         op0=ALU.add,
                         op1=ALU.mult,
@@ -228,7 +236,7 @@ def tile_attentionfreetransformerencoder_pb_kernel(
             for pair in range(PACK // 2):
                 bank = psum.tile([P, 2, 2 * P], F32, tag="x")
                 if pair == 0 and u >= 2:
-                    unread_passes(bank, 3)
+                    unread_passes(bank, 2)
                 for e in range(2):
                     for i in range(UNIT_TILES[u]):
                         nc.tensor.transpose(
@@ -278,8 +286,6 @@ def tile_attentionfreetransformerencoder_pb_kernel(
             banks = []
             for pair in range(PACK // 2):
                 bank = psum.tile([P, 2, 2 * P], F32, tag="q")
-                if pair == 0:
-                    unread_passes(bank, 3)
                 for e in range(2):
                     t = 2 * pair + e
                     nc.tensor.matmul_mx(
@@ -389,8 +395,8 @@ def tile_attentionfreetransformerencoder_pb_kernel(
                 h_quantised(j)
             if live(j):
                 q_transposed(j)
-            if live(j + 3):
-                normalise(j + 3)
+            if live(j + 2):
+                normalise(j + 2)
             if live(j + 2):
                 x_hat_transposed(j + 2)
             if live(j + 5):

@@ -99,12 +99,12 @@ def tile_attentionfreetransformerencoder_pb_kernel(
 
         for row in tiles_of(0):
             nc.sync.dma_start(out=x_all[:, row, :], in_=x_rows[:, row, :])
+        nc.sync.dma_start(out=bo_row[0:1, :], in_=bo.rearrange("(o n) -> o n", o=1))
         load_rows(x_all, x_rows, 1)
         nc.sync.dma_start(out=gain_bf[:], in_=ln1_g.rearrange("(p t) -> p t", t=PACK))
         nc.sync.dma_start(out=shift[:], in_=ln1_b.rearrange("(p t) -> p t", t=PACK))
         load_rows(x_all, x_rows, 2)
         load_rows(x_all, x_rows, 3)
-        nc.sync.dma_start(out=bo_row[0:1, :], in_=bo.rearrange("(o n) -> o n", o=1))
         load_weight(nc, Wq_words, Wq_scales, wq_words, wq_scales)
         nc.sync.dma_start(out=bq_col[:], in_=bq.rearrange("(p t) -> p t", t=PACK))
         load_rows(x_all, x_rows, 4)
@@ -159,8 +159,8 @@ def tile_attentionfreetransformerencoder_pb_kernel(
             moments_of[u] = moments
 
         def group_of(u):
-            first = u - (u - 1) % 2 if u >= 1 else u
-            last = min(first + 1, UNITS - 1) if u >= 1 else u
+            first = u - (u - 2) % 2 if u >= 2 else u
+            last = min(first + 1, UNITS - 1) if u >= 2 else u
             return first, last
 
         def aggregate(u):
@@ -395,9 +395,11 @@ def tile_attentionfreetransformerencoder_pb_kernel(
                 h_quantised(j)
             if live(j):
                 q_transposed(j)
-            if live(j + 2):
+            if j == -3:
+                normalise(0)
+                x_hat_transposed(0)
+            if live(j + 2) and j > -2:
                 normalise(j + 2)
-            if live(j + 2):
                 x_hat_transposed(j + 2)
             if live(j + 5):
                 stats(j + 5)
@@ -423,11 +425,11 @@ def tile_attentionfreetransformerencoder_pb_kernel(
                 residual(j + 1, "vector")
             if j == -4:
                 cast_gain()
-            if j == -2:
+            if j == -4:
                 spread_bo()
             if j == -1:
                 constants()
             if live(j + 1):
                 yt_transposed(j + 1)
-            if live(j + 1):
-                residual(j + 1, "gpsimd")
+            if live(j):
+                residual(j, "gpsimd")

from contextlib import ExitStack

import concourse.mybir as mybir
from concourse.masks import make_identity

F32 = mybir.dt.float32
BF16 = mybir.dt.bfloat16
I32 = mybir.dt.int32
U32 = mybir.dt.uint32
U8 = mybir.dt.uint8
FP8X4 = mybir.dt.float8_e4m3fn_x4
ACT = mybir.ActivationFunctionType
ALU = mybir.AluOpType

P = 128
D = 512
PACK = 4
ROWS = 2048
TILES = ROWS // P
UNIT_TILES = [2,2,2,2,2,2,2,2]
UNITS = len(UNIT_TILES)
FIRST_TILE = [sum(UNIT_TILES[:u]) for u in range(UNITS)]
QUADRANT = 32
QUADRANTS = P // QUADRANT
SCALE_ROWS = 4
BN_STATS_DIM = 6
BN_AGGR_DIM = 2
RUN = 4
EPS = 1e-5

FLOPS = 2 * 2 * ROWS * D * D


def norm_engine(u, i):
    return "vector"


def residual_engine(u, i):
    return "gpsimd"


def load_weight(nc, words_dram, scales_dram, words, scales):
    scale_rows = scales_dram.rearrange("g b n -> (g b) n")
    for quadrant in range(QUADRANTS):
        nc.sync.dma_start(
            out=scales[QUADRANT * quadrant : QUADRANT * quadrant + SCALE_ROWS, :].bitcast(I32),
            in_=scale_rows[SCALE_ROWS * quadrant : SCALE_ROWS * (quadrant + 1), :].bitcast(I32),
        )
    nc.sync.dma_start(
        out=words[:].bitcast(I32),
        in_=words_dram.rearrange("g p n t -> (g p) (n t)").bitcast(I32),
    )


def tile_attentionfreetransformerencoder_pb_kernel(
    tc, x, yt, ln1_g, ln1_b, Wq_words, Wq_scales, bq, Wo_words, Wo_scales, bo, out
):
    nc = tc.nc
    x_rows = x.flatten_outer_dims().rearrange("(p i) k -> p i k", i=TILES)
    yt_rows = yt.flatten_outer_dims().rearrange("(p i) k -> p i k", i=TILES)
    out_rows = out.flatten_outer_dims().rearrange("(p i) n -> p i n", i=TILES)

    with ExitStack() as ctx:
        keep = ctx.enter_context(tc.tile_pool(name="keep", bufs=1))
        small = ctx.enter_context(tc.tile_pool(name="small", bufs=UNITS))
        work = ctx.enter_context(tc.tile_pool(name="work", bufs=4))
        psum = ctx.enter_context(tc.psum_pool(name="psum", bufs=2))
        ctx.enter_context(tc.manual_schedule())

        wq_scales = keep.tile([P, D], U8, align_bytes=64)
        wo_scales = keep.tile([P, D], U8, align_bytes=64)
        nc.vector.memset(wq_scales[:].bitcast(I32), 0)
        nc.vector.memset(wo_scales[:].bitcast(I32), 0)
        wq_words = keep.tile([P, D * PACK], U8, align_bytes=64)
        wo_words = keep.tile([P, D * PACK], U8, align_bytes=64)
        wq_perm_words = keep.tile([P, D], I32, align_bytes=64)
        wq_perm_scales = keep.tile([P, D], U8, align_bytes=64)

        x_all = keep.tile([P, TILES, D], BF16)
        yt_all = keep.tile([P, TILES, D], BF16)
        x_bo = keep.tile([P, TILES, D], F32)

        def tiles_of(u):
            return range(FIRST_TILE[u], FIRST_TILE[u] + UNIT_TILES[u])

        def load_rows(dst, src, u):
            rows = slice(FIRST_TILE[u], FIRST_TILE[u] + UNIT_TILES[u])
            nc.sync.dma_start(out=dst[:, rows, :], in_=src[:, rows, :])

        gain_bf = keep.tile([P, PACK], BF16)
        shift = keep.tile([P, PACK], BF16)
        bq_col = keep.tile([P, PACK], BF16)
        bo_all = keep.tile([P, D], F32)

        bo_row = keep.tile([P, D], BF16)
        nc.gpsimd.memset(bo_row[:], 0.0)
        ones = keep.tile([P, P], BF16)
        nc.gpsimd.memset(ones[:], 1.0)

        for row in tiles_of(0):
            nc.sync.dma_start(out=x_all[:, row, :], in_=x_rows[:, row, :])
        nc.sync.dma_start(out=bo_row[0:1, :], in_=bo.rearrange("(o n) -> o n", o=1))
        load_rows(x_all, x_rows, 1)
        nc.sync.dma_start(out=gain_bf[:], in_=ln1_g.rearrange("(p t) -> p t", t=PACK))
        nc.sync.dma_start(out=shift[:], in_=ln1_b.rearrange("(p t) -> p t", t=PACK))
        load_rows(x_all, x_rows, 2)
        load_rows(x_all, x_rows, 3)
        load_weight(nc, Wq_words, Wq_scales, wq_words, wq_scales)
        nc.sync.dma_start(out=bq_col[:], in_=bq.rearrange("(p t) -> p t", t=PACK))
        load_rows(x_all, x_rows, 4)
        load_rows(yt_all, yt_rows, 0)
        load_rows(x_all, x_rows, 5)
        load_rows(yt_all, yt_rows, 1)
        load_weight(nc, Wo_words, Wo_scales, wo_words, wo_scales)
        for u in range(6, UNITS):
            load_rows(x_all, x_rows, u)
            load_rows(yt_all, yt_rows, u - 4)
        for u in range(UNITS - 4, UNITS):
            load_rows(yt_all, yt_rows, u)

        identity = keep.tile([P, P], F32)
        make_identity(nc, identity[:])
        minus_half = keep.tile([P, 4], F32)
        nc.gpsimd.memset(minus_half[:], -0.5)

        warm = keep.tile([P, 1], F32)
        nc.vector.memset(warm[:], 0.0)
        nc.scalar.activation(out=warm[:], in_=warm[:], func=ACT.Sigmoid)

        gain = keep.tile([P, PACK], F32)

        mean_var_of = {}
        mean_of = {}
        moments_of = {}
        minus_mean_rstd_of = {}
        rstd_of = {}
        x_hat_of = {}
        x_hat_t_of = {}
        h_by_t_of = {}
        h_grouped_of = {}
        h_quantised_of = {}
        q_t_of = {}
        sig_by_t_of = {}
        yt_t_of = {}
        y_grouped_of = {}
        y_quantised_of = {}
        o_bank_of = {}

        def spread_bo():
            bo_bank = psum.tile([P, D], F32, tag="o")
            nc.tensor.matmul(out=bo_bank[:], lhsT=ones[:], rhs=bo_row[:], start=True, stop=True)
            nc.scalar.copy(out=bo_all[:], in_=bo_bank[:])

        def stats(u):
            n = UNIT_TILES[u]
            moments = small.tile([P, 2, BN_STATS_DIM], F32)
            for i, row in enumerate(tiles_of(u)):
                nc.vector.bn_stats(out=moments[:, i, :], in_=x_all[:, row, :])
            moments_of[u] = moments

        def group_of(u):
            first = u - (u - 2) % 2 if u >= 2 else u
            last = min(first + 1, UNITS - 1) if u >= 2 else u
            return first, last

        def aggregate(u):
            first, last = group_of(u)
            if u == first:
                mean_var = small.tile([P, 4, BN_AGGR_DIM], F32)
                mean_var_of[first] = mean_var
            for i in range(2):
                nc.vector.bn_aggr(out=mean_var_of[first][:, 2 * (u - first) + i, :], in_=moments_of[u][:, i, :])
            if u < last:
                return
            n = 2 * (last - first + 1)
            mean_var = mean_var_of[first]
            var_eps = small.tile([P, 4], F32)
            rstd = small.tile([P, 4], F32)
            nc.gpsimd.tensor_scalar(
                out=var_eps[:, 0:n], in0=mean_var[:, 0:n, 1], scalar1=1.0, scalar2=EPS, op0=ALU.mult, op1=ALU.add
            )
            nc.gpsimd.tensor_tensor(out=rstd[:, 0:n], in0=var_eps[:, 0:n], in1=minus_half[:, 0:n], op=ALU.pow)
            minus_mean = small.tile([P, 4], F32)
            nc.gpsimd.tensor_scalar(
                out=minus_mean[:, 0:n], in0=mean_var[:, 0:n, 0], scalar1=-1.0, scalar2=0.0, op0=ALU.mult, op1=ALU.add
            )
            for v in range(first, last + 1):
                k = 2 * (v - first)
                rstd_of[v] = rstd[:, k : k + 2]
                mean_of[v] = minus_mean[:, k : k + 2]

        def normalise(u):
            x_hat = work.tile([P, 2, PACK, P], F32)
            for i, row in enumerate(tiles_of(u)):
                sorted_x = x_all[:, row, :].rearrange("r (p t) -> r t p", t=PACK)
                if norm_engine(u, i) == "scalar":
                    nc.scalar.activation(
                        out=x_hat[:, i, :, :],
                        in_=sorted_x,
                        func=ACT.Identity,
                        scale=rstd_of[u][:, i : i + 1],
                        bias=minus_mean_rstd_of[u][:, i : i + 1],
                    )
                else:
                    nc.vector.tensor_scalar(
                        out=x_hat[:, i, :, :],
                        in0=sorted_x,
                        scalar1=mean_of[u][:, i : i + 1],
                        scalar2=rstd_of[u][:, i : i + 1],
                        op0=ALU.add,
                        op1=ALU.mult,
                    )
            x_hat_of[u] = x_hat

        def residual(u, side):
            for i, row in enumerate(tiles_of(u)):
                if residual_engine(u, i) != side:
                    continue
                engine = nc.gpsimd if side == "gpsimd" else nc.vector
                engine.tensor_tensor(out=x_bo[:, row, :], in0=x_all[:, row, :], in1=bo_all[:], op=ALU.add)

        def unread_passes(bank, count):
            for n in range(count):
                nc.tensor.matmul_mx(
                    out=bank[:].rearrange("p e r -> p (e r)"),
                    lhsT=wq_perm_words[:, 0:P].bitcast(FP8X4),
                    lhsT_scale=wq_perm_scales[:, 0:P],
                    rhs=wq_words[:].bitcast(FP8X4),
                    rhs_scale=wq_scales[:],
                    start=True,
                    stop=True,
                )

        def x_hat_transposed(u):
            banks = []
            for pair in range(PACK // 2):
                bank = psum.tile([P, 2, 2 * P], F32, tag="x")
                if pair == 0 and u >= 2:
                    unread_passes(bank, 2)
                for e in range(2):
                    for i in range(UNIT_TILES[u]):
                        nc.tensor.transpose(
                            bank[:, e, i * P : (i + 1) * P], x_hat_of[u][:, i, 2 * pair + e, :], identity[:]
                        )
                banks.append(bank)
            x_hat_t_of[u] = banks

        def h_by_t(u):
            rows = UNIT_TILES[u] * P
            by_t = work.tile([P, PACK, rows], BF16, name="h_by_t_%d" % rows)
            for t in range(PACK):
                nc.scalar.activation(
                    out=by_t[:, t, :],
                    in_=x_hat_t_of[u][t // 2][:, t % 2, 0:rows],
                    func=ACT.Identity,
                    scale=gain[:, t : t + 1],
                    bias=shift[:, t : t + 1],
                )
            h_by_t_of[u] = by_t

        def h_grouped(u):
            rows = UNIT_TILES[u] * P
            grouped = work.tile([P, rows, PACK], BF16, align_bytes=64, name="h_grouped_%d" % rows)
            nc.scalar.copy(
                out=grouped[:].rearrange("p (c i) t -> p c t i", i=RUN),
                in_=h_by_t_of[u][:].rearrange("p t (c i) -> p c t i", i=RUN),
            )
            h_grouped_of[u] = grouped

        def quantise(grouped, rows, name):
            words = work.tile([P, rows], U32, align_bytes=64, name="%s_words_%d" % (name, rows))
            scales = work.tile([P, rows], U8, align_bytes=64, name="%s_scales_%d" % (name, rows))
            nc.vector.quantize_mx(
                out=words[:].bitcast(FP8X4),
                scales=scales[:],
                in_=grouped[:].rearrange("p r t -> p (r t)"),
            )
            return words, scales

        def h_quantised(u):
            h_quantised_of[u] = quantise(h_grouped_of[u], UNIT_TILES[u] * P, "h")

        def q_transposed(u):
            rows = UNIT_TILES[u] * P
            words, scales = h_quantised_of[u]
            banks = []
            for pair in range(PACK // 2):
                bank = psum.tile([P, 2, 2 * P], F32, tag="q")
                for e in range(2):
                    t = 2 * pair + e
                    nc.tensor.matmul_mx(
                        out=bank[:, e, 0:rows],
                        lhsT=wq_perm_words[:, t * P : (t + 1) * P].bitcast(FP8X4),
                        lhsT_scale=wq_perm_scales[:, t * P : (t + 1) * P],
                        rhs=words[:].bitcast(FP8X4),
                        rhs_scale=scales[:],
                        start=True,
                        stop=True,
                    )
                banks.append(bank)
            q_t_of[u] = banks

        def parts(u):
            return [(0, 1), (1, 1)] if u == UNITS - 1 else [(0, UNIT_TILES[u])]

        def sigmoid_by_t(u, first, n):
            rows = n * P
            sig_by_t = work.tile([P, PACK, rows], F32, name="sig_by_t_%d" % rows)
            for t in range(PACK):
                nc.scalar.activation(
                    out=sig_by_t[:, t, :],
                    in_=q_t_of[u][t // 2][:, t % 2, first * P : first * P + rows],
                    func=ACT.Sigmoid,
                    bias=bq_col[:, t : t + 1],
                )
            sig_by_t_of[u, first] = sig_by_t

        def yt_transposed(u):
            n = UNIT_TILES[u]
            yt_t = psum.tile([P, 4 * P], F32, tag="yt")
            for w in range(2):
                for i, row in enumerate(tiles_of(u)):
                    yt_words = yt_all[:, row, :].bitcast(F32).rearrange("r (p w) -> r w p", w=2)
                    nc.tensor.transpose(
                        yt_t[:, 2 * i * P : 2 * (i + 1) * P].rearrange("p (r w) -> p w r", w=2)[:, w, :],
                        yt_words[:, w, :],
                        identity[:],
                    )
            yt_t_of[u] = yt_t

        def y_grouped(u, first, n):
            rows = n * P
            grouped = work.tile([P, rows, PACK], BF16, align_bytes=64, name="y_grouped_%d" % rows)
            nc.vector.tensor_tensor(
                out=grouped[:].rearrange("p (c i) t -> p c t i", i=RUN),
                in0=sig_by_t_of[u, first][:].rearrange("p t (c i) -> p c t i", i=RUN),
                in1=yt_t_of[u][:, 2 * first * P : 2 * first * P + 2 * rows].bitcast(BF16).rearrange("p (c i t) -> p c t i", i=RUN, t=PACK),
                op=ALU.mult,
            )
            y_grouped_of[u, first] = grouped

        def y_quantised(u, first, n):
            y_quantised_of[u, first] = quantise(y_grouped_of[u, first], n * P, "y")

        def projected(u, first, n):
            words, scales = y_quantised_of[u, first]
            banks = []
            for i in range(n):
                o_bank = psum.tile([P, D], F32, tag="o")
                nc.tensor.matmul_mx(
                    out=o_bank[:],
                    lhsT=words[:, i * P : (i + 1) * P].bitcast(FP8X4),
                    lhsT_scale=scales[:, i * P : (i + 1) * P],
                    rhs=wo_words[:].bitcast(FP8X4),
                    rhs_scale=wo_scales[:],
                    start=True,
                    stop=True,
                )
                banks.append(o_bank)
            o_bank_of[u] = o_bank_of.get(u, []) + banks

        def stored(u):
            for i, row in enumerate(tiles_of(u)):
                o_sb = work.tile([P, D], F32)
                pieces = 2 if row == TILES - 1 else 1
                for piece in range(pieces):
                    columns = slice(piece * D // pieces, (piece + 1) * D // pieces)
                    nc.vector.tensor_tensor(
                        out=o_sb[:, columns], in0=o_bank_of[u][i][:, columns], in1=x_bo[:, row, columns], op=ALU.add
                    )
                    nc.sync.dma_start(out=out_rows[:, row, columns], in_=o_sb[:, columns])

        def cast_gain():
            nc.vector.tensor_copy(out=gain[:], in_=gain_bf[:])

        def constants():
            nc.vector.tensor_copy(
                out=wq_perm_words[:].rearrange("p (t m) -> p t m", t=PACK),
                in_=wq_words[:].bitcast(I32).rearrange("p (m t) -> p t m", t=PACK),
            )
            nc.vector.tensor_copy(
                out=wq_perm_scales[:].rearrange("p (t m) -> p t m", t=PACK),
                in_=wq_scales[:].rearrange("p (m t) -> p t m", t=PACK),
            )

        def live(u):
            return 0 <= u < UNITS

        for j in range(-5, UNITS + 2):
            if live(j + 1):
                h_by_t(j + 1)
            if live(j + 1):
                h_grouped(j + 1)
            if live(j):
                h_quantised(j)
            if live(j):
                q_transposed(j)
            if j == -3:
                normalise(0)
                x_hat_transposed(0)
            if live(j + 2) and j > -2:
                normalise(j + 2)
                x_hat_transposed(j + 2)
            if live(j + 5):
                stats(j + 5)
            if live(j - 1):
                for part in parts(j - 1):
                    y_grouped(j - 1, *part)
            if live(j - 2) and j != UNITS:
                stored(j - 2)
            if live(j + 5):
                aggregate(j + 5)
            if live(j - 1):
                for part in parts(j - 1):
                    y_quantised(j - 1, *part)
            if live(j - 1):
                for part in parts(j - 1):
                    projected(j - 1, *part)
            if j == UNITS:
                stored(j - 2)
            if live(j):
                for part in parts(j):
                    sigmoid_by_t(j, *part)
            if live(j + 1):
                residual(j + 1, "vector")
            if j == -4:
                cast_gain()
            if j == -4:
                spread_bo()
            if j == -1:
                constants()
            if live(j + 1):
                yt_transposed(j + 1)
            if live(j):
                residual(j, "gpsimd")
